import numpy as np
import ml_dtypes


def mxq(x, axis, fmt="e4m3"):
    dtype, down = {"e4m3": (ml_dtypes.float8_e4m3fn, 7), "e5m2": (ml_dtypes.float8_e5m2, 14)}[fmt]
    v = np.moveaxis(np.asarray(x, np.float32).astype(ml_dtypes.bfloat16).astype(np.float64), axis, -1)
    blocks = v.reshape(v.shape[:-1] + (-1, 32))
    amax = np.abs(blocks).max(-1, keepdims=True)
    byte = np.maximum(np.where(amax > 0, np.frexp(amax)[1] - 1 + 127, 0) - down, 1)
    scale = np.exp2(byte - 127.0)
    codes = (blocks / scale).astype(np.float32).astype(dtype).astype(np.float64)
    return np.moveaxis((codes * scale).reshape(v.shape), -1, axis)


WIDE = False


def mx_kscale(k):
    if not WIDE:
        return np.ones(k)
    levels = np.array([10, -10, 5, -5, 0])
    if k % 512:
        return np.exp2(np.random.permutation(np.resize(levels, k // 32))).repeat(32)
    a = np.empty((k // 512, 16))
    for p in range(k // 512):
        a[p, :8] = np.random.permutation(np.resize(levels, 8))
        for g in range(8):
            far = levels[np.abs(levels - a[p, g]) >= 10]
            a[p, g + 8] = far[np.random.randint(len(far))]
    return np.exp2(a.ravel()).repeat(32)


BF16 = ml_dtypes.bfloat16


def bf(x):
    return np.asarray(x, np.float32).astype(BF16)


def f64(x):
    return np.asarray(x).astype(np.float64)


E2M1 = np.array([0.0, 0.5, 1.0, 1.5, 2.0, 3.0, 4.0, 6.0, -0.0, -0.5, -1.0, -1.5, -2.0, -3.0, -4.0, -6.0])


def pack_weight(w, fmt):
    k, n = w.shape
    w = f64(bf(w)).reshape(k // 32, 32, n)
    amax = np.abs(w).max(1)
    if fmt == "e4m3":
        byte = np.frexp(amax)[1] - 1 + 127 - 7
    else:
        mant, ex = np.frexp(amax / 6.0)
        byte = np.where(mant > 0.5, ex, ex - 1) + 127
    byte = np.clip(np.where(amax > 0, byte, 1), 1, 254)
    scaled = (w * np.exp2(127.0 - byte)[:, None, :]).reshape(k, n).astype(np.float32)
    by_word = np.ascontiguousarray(scaled.reshape(k // 512, 128, 4, n).transpose(0, 1, 3, 2))
    if fmt == "e4m3":
        words = by_word.astype(ml_dtypes.float8_e4m3fn).view(np.uint8)
    else:
        c = by_word.astype(ml_dtypes.float4_e2m1fn).view(np.uint8) & 0xF
        words = c[..., 0::2] | (c[..., 1::2] << 4)
    return np.ascontiguousarray(words), np.ascontiguousarray(byte.astype(np.uint8).reshape(k // 512, 16, n))


def unpack_weight(words, scales, fmt):
    g, p, n, _ = words.shape
    if fmt == "e4m3":
        vals = np.ascontiguousarray(words).view(ml_dtypes.float8_e4m3fn).astype(np.float64)
    else:
        nib = np.empty((g, p, n, 4), np.uint8)
        nib[..., 0::2] = words & 0xF
        nib[..., 1::2] = words >> 4
        vals = E2M1[nib]
    vals = vals * np.repeat(np.exp2(scales.astype(np.float64) - 127.0), 8, axis=1)[..., None]
    return vals.transpose(0, 1, 3, 2).reshape(g * 512, n)
def pack4(w):
    words, scales = pack_weight(w, "e2m1")
    return words.reshape(words.shape[0], 128, -1), scales


def unpack4(words, scales):
    return unpack_weight(words.reshape(words.shape[0], 128, -1, 2), scales, "e2m1")


N, IN_DIM, HID, OUT_DIM = 1024, 1024, 512, 256
CAT = 3 * HID


def log_softmax(v):
    d = v - v.max(-1, keepdims=True)
    return d - np.log(np.exp(d).sum(-1, keepdims=True))


def draw0():
    s, t = mx_kscale(HID), mx_kscale(CAT)
    ta, tb, tc = t[:HID], t[HID:2 * HID], t[2 * HID:]
    u1 = bf(np.maximum(np.random.standard_normal((N, HID)) * 2.0, 0.0) * s)
    W2_1_words, W2_1_scales = pack4(np.random.standard_normal((HID, HID)) * 0.5 / np.sqrt(HID) / s[:, None] * tc)
    b2_1 = bf(np.random.standard_normal(HID) * 0.3 * tc)
    h = bf(np.random.standard_normal((N, HID)) * ta)
    h1 = bf(np.random.standard_normal((N, HID)) * 0.8 * tb)
    W_out_words, W_out_scales = pack4(np.random.standard_normal((CAT, OUT_DIM)) * 2.0 / np.sqrt(CAT) / t[:, None])
    b_out = bf(np.random.standard_normal(OUT_DIM) * 0.3)
    return {"u1": u1,
            "W2_1_words": W2_1_words,
            "W2_1_scales": W2_1_scales,
            "b2_1": b2_1,
            "h": h,
            "h1": h1,
            "W_out_words": W_out_words,
            "W_out_scales": W_out_scales,
            "b_out": b_out}


def core(u1, W2_1_words, W2_1_scales, b2_1, h, h1, W_out_words, W_out_scales, b_out):
    h2 = (mxq(f64(u1), 1, "e4m3") @ unpack4(W2_1_words, W2_1_scales)) + f64(b2_1)
    cat = np.concatenate([f64(h), f64(h1), h2], axis=-1)
    logits = (mxq(cat, 1, "e4m3") @ unpack4(W_out_words, W_out_scales)) + f64(b_out)
    return log_softmax(logits)


def e4m3fn_bytes(y):
    return np.clip(np.asarray(y, np.float64), -448.0, 448.0).astype(np.float32).astype(ml_dtypes.float8_e4m3fn).view(np.uint8)


def e4m3fn_values(b):
    return np.asarray(b, np.uint8).view(ml_dtypes.float8_e4m3fn).astype(np.float64)


def setup_inputs():
    d = draw0()
    x0 = np.asarray(d['u1']).astype(np.float64)
    s = (np.max(np.abs(x0), axis=(0,), keepdims=True) / 448.0).astype(np.float32)
    out = {}
    for k, v in d.items():
        if k == 'u1':
            out['u1_bytes'] = e4m3fn_bytes(x0 / s.astype(np.float64))
            out['u1_scale'] = s
        else:
            out[k] = v
    return out


def reference(u1_bytes, u1_scale, W2_1_words, W2_1_scales, b2_1, h, h1, W_out_words, W_out_scales, b_out):
    return core(e4m3fn_values(u1_bytes) * u1_scale.astype(np.float64), W2_1_words, W2_1_scales, b2_1, h, h1, W_out_words, W_out_scales, b_out)

@@ -1,0 +1,413 @@
+from contextlib import ExitStack
+
+import concourse.mybir as mybir
+from concourse.masks import make_identity
+
+FLOPS = 2 * 1024 * 512 * 512 + 2 * 1024 * 1536 * 256
+
+F32 = mybir.dt.float32
+BF16 = mybir.dt.bfloat16
+I32 = mybir.dt.int32
+U32 = mybir.dt.uint32
+U8 = mybir.dt.uint8
+FP8 = mybir.dt.float8_e4m3fn
+FP8X4 = mybir.dt.float8_e4m3fn_x4
+FP4X4 = mybir.dt.float4_e2m1fn_x4
+ADD = mybir.AluOpType.add
+SUB = mybir.AluOpType.subtract
+MULT = mybir.AluOpType.mult
+MAX = mybir.AluOpType.max
+AX = mybir.AxisListType.X
+EXP = mybir.ActivationFunctionType.Exp
+LN = mybir.ActivationFunctionType.Ln
+IDENT = mybir.ActivationFunctionType.Identity
+
+P = 128
+NODES, HID, CLS = 1024, 512, 256
+NB = NODES // P
+NP = NB // 2
+BOTH = slice(0, 2)
+
+
+def tile_gin_pc_w4_kernel(
+    tc, u1_bytes, u1_scale, w2_words, w2_scales, b2_1, h, h1, wo_words, wo_scales, b_out, out
+):
+    nc = tc.nc
+    with ExitStack() as ctx:
+        keep = ctx.enter_context(tc.tile_pool(name="keep", bufs=1))
+        tr_pool = ctx.enter_context(tc.psum_pool(name="tr_pool", bufs=4))
+        h2_pool = ctx.enter_context(tc.psum_pool(name="h2_pool", bufs=2))
+        lg_pool = ctx.enter_context(tc.psum_pool(name="lg_pool", bufs=2))
+        ctx.enter_context(tc.manual_schedule())
+
+        def sb(shape, dtype, name):
+            return keep.tile(shape, dtype, name=name, align_bytes=64)
+
+        scale_col = sb([P, 4], F32, "scale_col")
+        bo_col = sb([P, 2], BF16, "bo_col")
+        b2_col = sb([P, 4], BF16, "b2_col")
+        u_raw = [sb([P, 4, HID], U8, f"u_raw{c}") for c in range(2)]
+        h_sb = [sb([P, 4, HID], BF16, f"h_sb{c}") for c in range(2)]
+        g_sb = [sb([P, 4, HID], BF16, f"g_sb{c}") for c in range(2)]
+
+        def block(tiles, n):
+            return tiles[n // 4][:, n % 4, :]
+
+        w2_in = sb([P, 2 * HID], U8, "w2_in")
+        w2_perm = sb([P, 2 * HID], U8, "w2_perm")
+        w2s_in = sb([P, HID], U8, "w2s_in")
+        w2s_perm = sb([P, HID], U8, "w2s_perm")
+        wo = sb([P, 3, 2 * CLS], U8, "wo")
+        wos = sb([P, 3, CLS], U8, "wos")
+        ident = sb([P, P], F32, "ident")
+        scale_all = sb([P, 2, HID], F32, "scale_all")
+        bo_all = sb([P, CLS], BF16, "bo_all")
+        u_val = [sb([P, 2, HID], BF16, f"u_val{i}") for i in range(NP)]
+        u_grp = [sb([P, 256, 4], BF16, f"u_grp{i}") for i in range(NP)]
+        hg_grp = [sb([P, 2, 256, 4], BF16, f"hg_grp{i}") for i in range(NP)]
+        h2_flat = [sb([P, 4, 256], BF16, f"h2_flat{i}") for i in range(NP)]
+        h2_grp = [sb([P, 256, 4], BF16, f"h2_grp{i}") for i in range(NP)]
+        u_codes = [sb([P, 256], U32, f"u_codes{i}") for i in range(NP)]
+        u_scl = [sb([P, 256], U8, f"u_scl{i}") for i in range(NP)]
+        hg_codes = [sb([P, 512], U32, f"hg_codes{i}") for i in range(NP)]
+        hg_scl = [sb([P, 512], U8, f"hg_scl{i}") for i in range(NP)]
+        h2_codes = [sb([P, 256], U32, f"h2_codes{i}") for i in range(NP)]
+        h2_scl = [sb([P, 256], U8, f"h2_scl{i}") for i in range(NP)]
+        logits = [sb([P, 2, CLS], F32, f"logits{i}") for i in range(NP)]
+        junk = sb([P, CLS], F32, "junk")
+        nmax = sb([P, NB], F32, "nmax")
+        ssum = sb([P, NB], F32, "ssum")
+        lns = sb([P, NB], F32, "lns")
+        res = [sb([P, 2, CLS], F32, f"res{i}") for i in range(NP)]
+        warm = sb([P, 1], F32, "warm")
+
+        u_hbm = u1_bytes.rearrange("(p b) k -> p b k", b=NB)
+        h_hbm = h.rearrange("(p b) k -> p b k", b=NB)
+        g_hbm = h1.rearrange("(p b) k -> p b k", b=NB)
+        o_hbm = out.rearrange("(p b) c -> p b c", b=NB)
+
+        def load_u(i):
+            nc.sync.dma_start(out=u_raw[i][:], in_=u_hbm[:, 4 * i : 4 * i + 4, :])
+
+        def load_h(i):
+            nc.sync.dma_start(out=h_sb[i][:], in_=h_hbm[:, 4 * i : 4 * i + 4, :])
+
+        def load_g(i):
+            nc.sync.dma_start(out=g_sb[i][:], in_=g_hbm[:, 4 * i : 4 * i + 4, :])
+
+        make_identity(nc, ident[:])
+        nc.vector.memset(warm[:], 0.0)
+        nc.vector.memset(w2s_in[:].bitcast(I32), 0)
+        nc.vector.memset(wos[:].rearrange("p g n -> p (g n)").bitcast(I32), 0)
+
+        nc.sync.dma_start(out=w2_in[:], in_=w2_words[0])
+        nc.sync.dma_start(out=scale_col[:], in_=u1_scale.rearrange("o (p j) -> p (o j)", j=4))
+        w2s_hbm = w2_scales[0].rearrange("(q r) n -> r q n", r=4)
+        for r in range(4):
+            nc.sync.dma_start(out=w2s_in[r:P:32, :].bitcast(I32), in_=w2s_hbm[r].bitcast(I32))
+        load_u(0)
+        load_h(0)
+        load_g(0)
+        load_u(1)
+        nc.sync.dma_start(out=b2_col[:], in_=b2_1.rearrange("(p t) -> p t", t=4))
+        load_h(1)
+        load_g(1)
+        nc.sync.dma_start(out=wo[:], in_=wo_words.rearrange("g p n -> p g n"))
+        nc.sync.dma_start(out=bo_col[:], in_=b_out.rearrange("(p t) -> p t", t=2))
+        wos_hbm = wo_scales.rearrange("g (q r) n -> r q g n", r=4)
+        for r in range(4):
+            nc.sync.dma_start(out=wos[r:P:32, :, :].bitcast(I32), in_=wos_hbm[r].bitcast(I32))
+
+        nc.scalar.activation(out=warm[:], in_=warm[:], func=EXP)
+
+        def spread_scale():
+            bank = tr_pool.tile([P, 4, P], F32, name="bank", tag="tr")
+            for j in range(4):
+                nc.tensor.transpose(bank[:, j, :], scale_col[:, j : j + 1].to_broadcast([P, P]), ident[:])
+            for c in range(2):
+                nc.scalar.copy(
+                    out=scale_all[:, c, :].rearrange("p (n j) -> p n j", j=4),
+                    in_=bank[:].rearrange("p j n -> p n j"),
+                )
+
+        def spread_b_out():
+            bank = tr_pool.tile([P, P], F32, name="bank", tag="tr")
+            nc.tensor.transpose(bank[:], bo_col[:].bitcast(F32).to_broadcast([P, P]), ident[:])
+            nc.scalar.copy(out=bo_all[:].bitcast(F32), in_=bank[:])
+
+        def permute_w2_words():
+            nc.vector.tensor_copy(
+                out=w2_perm[:].rearrange("p (t m b) -> p t m b", t=4, b=2),
+                in_=w2_in[:].rearrange("p (m t b) -> p t m b", t=4, b=2),
+            )
+
+        def permute_w2_scales():
+            nc.vector.tensor_copy(
+                out=w2s_perm[:].rearrange("p (t m) -> p t m", t=4),
+                in_=w2s_in[:].rearrange("p (m t) -> p t m", t=4),
+            )
+
+        def widen(i, b):
+            nc.vector.tensor_tensor(
+                out=u_val[i][:, b, :], in0=block(u_raw, 2 * i + b).bitcast(FP8), in1=scale_all[:, 0, :], op=MULT
+            )
+
+        def widen_pair(i):
+            c, b0 = i // 2, 2 * (i % 2)
+            nc.vector.tensor_tensor(
+                out=u_val[i][:].rearrange("p b k -> p (b k)"),
+                in0=u_raw[c][:, b0 : b0 + 2, :].rearrange("p b k -> p (b k)").bitcast(FP8),
+                in1=scale_all[:].rearrange("p b k -> p (b k)"),
+                op=MULT,
+            )
+
+        banks = {}
+
+        def source(x, i, b):
+            if x == "u":
+                return u_val[i][:, b, :]
+            return block(h_sb if x == "h" else g_sb, 2 * i + b)
+
+        def turn(x, i):
+            bank = tr_pool.tile([P, 2, 2, P], F32, name="bank", tag="tr")
+            banks[x, i] = bank
+            for b in range(2):
+                words = source(x, i, b).bitcast(F32)
+                for e in range(2):
+                    nc.tensor.transpose(bank[:, b, e, :], words[:, e : HID // 2 : 2], ident[:])
+
+        def group(x, i):
+            dst = u_grp[i][:] if x == "u" else hg_grp[i][:, 0 if x == "h" else 1]
+            nc.scalar.copy(
+                out=dst.rearrange("p (b n) t -> p b n t", b=2).bitcast(F32),
+                in_=banks[x, i][:].rearrange("p b e n -> p b n e"),
+            )
+
+        def quantize(codes, scl, grp):
+            nc.vector.quantize_mx(out=codes[:].bitcast(FP8X4), scales=scl[:], in_=grp)
+
+        def quantize_u(i):
+            quantize(u_codes[i], u_scl[i], u_grp[i][:].rearrange("p n t -> p (n t)"))
+
+        def quantize_hg(i):
+            quantize(hg_codes[i], hg_scl[i], hg_grp[i][:].rearrange("p s n t -> p (s n t)"))
+
+        def quantize_h2(i):
+            quantize(h2_codes[i], h2_scl[i], h2_grp[i][:].rearrange("p n t -> p (n t)"))
+
+        def matmul_h2(i, b):
+            bank = h2_pool.tile([P, 4, P], F32, name="h2_bank", tag="h2")
+            banks["h2", i, b] = bank
+            nodes = slice(b * P, (b + 1) * P)
+            for t in range(4):
+                nc.tensor.matmul_mx(
+                    out=bank[:, t, :],
+                    lhsT=w2_perm[:, 2 * P * t : 2 * P * (t + 1)].bitcast(FP4X4),
+                    lhsT_scale=w2s_perm[:, P * t : P * (t + 1)],
+                    rhs=u_codes[i][:, nodes].bitcast(FP8X4),
+                    rhs_scale=u_scl[i][:, nodes],
+                    start=True,
+                    stop=True,
+                )
+
+        def bias_h2(i, b):
+            nc.vector.tensor_tensor(
+                out=h2_grp[i][:, b * P : (b + 1) * P, :],
+                in0=banks["h2", i, b][:].rearrange("p t n -> p n t"),
+                in1=b2_col[:].unsqueeze(1).to_broadcast([P, P, 4]),
+                op=ADD,
+            )
+
+        def matmul_h2_pair(i):
+            for u in range(2):
+                bank = h2_pool.tile([P, 2, 256], F32, name="h2_bank", tag="h2")
+                banks["h2", i, u] = bank
+                for v in range(2):
+                    t = 2 * u + v
+                    nc.tensor.matmul_mx(
+                        out=bank[:, v, :],
+                        lhsT=w2_perm[:, 2 * P * t : 2 * P * (t + 1)].bitcast(FP4X4),
+                        lhsT_scale=w2s_perm[:, P * t : P * (t + 1)],
+                        rhs=u_codes[i][:].bitcast(FP8X4),
+                        rhs_scale=u_scl[i][:],
+                        start=True,
+                        stop=True,
+                    )
+
+        def bias_h2_scalar(i):
+            for t in range(4):
+                nc.scalar.activation(
+                    out=h2_flat[i][:, t, :],
+                    in_=banks["h2", i, t // 2][:, t % 2, :],
+                    func=IDENT,
+                    bias=b2_col[:, t : t + 1],
+                )
+
+        def interleave_h2(i):
+            nc.vector.tensor_copy(out=h2_grp[i][:], in_=h2_flat[i][:].rearrange("p t n -> p n t"))
+
+        def cat_codes(i, g, b):
+            n0 = (g * 256 if g < 2 else 0) + b * P
+            codes, scl = (hg_codes[i], hg_scl[i]) if g < 2 else (h2_codes[i], h2_scl[i])
+            return codes[:, n0 : n0 + P].bitcast(FP8X4), scl[:, n0 : n0 + P]
+
+        def wo_codes(g, c):
+            return wo[:, g, 2 * P * c : 2 * P * (c + 1)].bitcast(FP4X4), wos[:, g, c * P : (c + 1) * P]
+
+        def matmul_out(i):
+            bank = lg_pool.tile([P, 2, CLS], F32, name="lg_bank", tag="lg")
+            banks["lg", i] = bank
+            for b in range(2):
+                for c in range(2):
+                    for g in range(3):
+                        x, xs = cat_codes(i, g, b)
+                        w, ws = wo_codes(g, c)
+                        nc.tensor.matmul_mx(
+                            out=bank[:, b, c * P : (c + 1) * P],
+                            lhsT=x, lhsT_scale=xs, rhs=w, rhs_scale=ws,
+                            start=(g == 0), stop=(g == 2),
+                        )
+
+        def bias_out(i, blocks=BOTH):
+            nc.vector.tensor_tensor(
+                out=logits[i][:, blocks, :],
+                in0=banks["lg", i][:, blocks, :],
+                in1=bo_all[:].unsqueeze(1).to_broadcast([P, blocks.stop - blocks.start, CLS]),
+                op=ADD,
+            )
+
+        def row_max(i, blocks=BOTH):
+            nc.vector.tensor_reduce(
+                out=nmax[:, 2 * i + blocks.start : 2 * i + blocks.stop],
+                in_=logits[i][:, blocks, :],
+                axis=AX,
+                op=MAX,
+                negate=True,
+            )
+
+        def exp_sum(i, b):
+            n = 2 * i + b
+            nc.scalar.activation(
+                out=junk[:],
+                in_=logits[i][:, b, :],
+                func=EXP,
+                bias=nmax[:, n : n + 1],
+                accum_out=ssum[:, n : n + 1],
+            )
+
+        def log_sum(b0, b1):
+            nc.scalar.activation(out=lns[:, b0:b1], in_=ssum[:, b0:b1], func=LN)
+
+        def finish(i, b):
+            n = 2 * i + b
+            nc.vector.tensor_scalar(
+                out=res[i][:, b, :],
+                in0=logits[i][:, b, :],
+                scalar1=nmax[:, n : n + 1],
+                scalar2=lns[:, n : n + 1],
+                op0=ADD,
+                op1=SUB,
+            )
+
+        def store(i, b):
+            nc.sync.dma_start(out=o_hbm[:, 2 * i + b, :], in_=res[i][:, b, :])
+
+        permute_w2_words()
+        spread_scale()
+        turn("h", 0)
+        permute_w2_scales()
+        widen(0, 0)
+        widen(0, 1)
+        group("h", 0)
+        widen_pair(1)
+        turn("h", 1)
+        group("h", 1)
+        turn("u", 0)
+        widen_pair(2)
+        turn("g", 0)
+        turn("u", 1)
+        group("u", 0)
+        turn("g", 1)
+        turn("u", 2)
+        group("u", 1)
+        quantize_u(0)
+        widen_pair(3)
+        group("g", 1)
+        quantize_u(1)
+        matmul_h2(0, 1)
+        group("g", 0)
+        matmul_h2(0, 0)
+        spread_b_out()
+        bias_h2(0, 0)
+        bias_h2(0, 1)
+        group("u", 2)
+        quantize_hg(0)
+        turn("h", 2)
+        group("h", 2)
+        turn("u", 3)
+        group("u", 3)
+        quantize_h2(0)
+        quantize_u(3)
+        matmul_h2_pair(1)
+        quantize_u(2)
+        bias_h2_scalar(1)
+        matmul_out(0)
+        quantize_hg(1)
+        turn("g", 2)
+        group("g", 2)
+        interleave_h2(1)
+        bias_out(0, slice(0, 2))
+        quantize_h2(1)
+        row_max(0, slice(0, 2))
+        matmul_h2_pair(2)
+        bias_h2_scalar(2)
+        quantize_hg(2)
+        matmul_out(1)
+        bias_out(1, slice(0, 2))
+        turn("g", 3)
+        turn("h", 3)
+        interleave_h2(2)
+        row_max(1, slice(0, 2))
+        exp_sum(0, 0)
+        exp_sum(0, 1)
+        quantize_h2(2)
+        matmul_h2(3, 0)
+        group("g", 3)
+        group("h", 3)
+        matmul_h2(3, 1)
+        matmul_out(2)
+        bias_h2(3, 0)
+        bias_h2(3, 1)
+        quantize_hg(3)
+        quantize_h2(3)
+        bias_out(2, slice(0, 2))
+        exp_sum(1, 0)
+        exp_sum(1, 1)
+        matmul_out(3)
+        bias_out(3, slice(0, 1))
+        row_max(2, slice(0, 2))
+        log_sum(0, 4)
+        exp_sum(2, 0)
+        exp_sum(2, 1)
+        row_max(3, slice(0, 1))
+        exp_sum(3, 0)
+        bias_out(3, slice(1, 2))
+        row_max(3, slice(1, 2))
+        exp_sum(3, 1)
+        finish(0, 0)
+        finish(0, 1)
+        store(0, 0)
+        finish(1, 0)
+        finish(1, 1)
+        store(1, 1)
+        store(0, 1)
+        store(1, 0)
+        log_sum(4, 8)
+        finish(3, 0)
+        finish(2, 1)
+        store(3, 0)
+        finish(2, 0)
+        store(2, 1)
+        store(2, 0)
+        finish(3, 1)
+        store(3, 1)

@@ -1,3 +1,4 @@
+import math
 from contextlib import ExitStack
 
 import concourse.mybir as mybir
@@ -14,19 +15,26 @@ FP8 = mybir.dt.float8_e4m3fn
 FP8X4 = mybir.dt.float8_e4m3fn_x4
 FP4X4 = mybir.dt.float4_e2m1fn_x4
 ADD = mybir.AluOpType.add
-SUB = mybir.AluOpType.subtract
 MULT = mybir.AluOpType.mult
 MAX = mybir.AluOpType.max
 AX = mybir.AxisListType.X
 EXP = mybir.ActivationFunctionType.Exp
-LN = mybir.ActivationFunctionType.Ln
 IDENT = mybir.ActivationFunctionType.Identity
 
 P = 128
 NODES, HID, CLS = 1024, 512, 256
 NB = NODES // P
 NP = NB // 2
-BOTH = slice(0, 2)
+
+LOG_STEP = -0.875
+STEP = math.exp(LOG_STEP)
+TERMS = 50
+T0 = 3.25 - (TERMS - 1) * STEP
+T_TAIL = T0 + STEP - math.log(math.exp(STEP) - 1.0)
+LOG_CONST = STEP * (math.exp(-math.exp(T_TAIL)) + sum(math.exp(-math.exp(T0 + j * STEP)) for j in range(1, TERMS)))
+
+U_LOADS = ((0, 1), (1, 1), (2, 2))
+HG_LOADS = ((0, 1), (1, 1), (2, 1), (3, 1))
 
 
 def tile_gin_pc_w4_kernel(
@@ -44,14 +52,14 @@ def tile_gin_pc_w4_kernel(
             return keep.tile(shape, dtype, name=name, align_bytes=64)
 
         scale_col = sb([P, 4], F32, "scale_col")
-        bo_col = sb([P, 2], BF16, "bo_col")
         b2_col = sb([P, 4], BF16, "b2_col")
-        u_raw = [sb([P, 4, HID], U8, f"u_raw{c}") for c in range(2)]
-        h_sb = [sb([P, 4, HID], BF16, f"h_sb{c}") for c in range(2)]
-        g_sb = [sb([P, 4, HID], BF16, f"g_sb{c}") for c in range(2)]
+        u_raw = {i: sb([P, n, 2 * HID], U8, f"u_raw{i}") for i, n in U_LOADS}
+        h_sb = {i: sb([P, n, HID], F32, f"h_sb{i}") for i, n in HG_LOADS}
+        g_sb = {i: sb([P, n, HID], F32, f"g_sb{i}") for i, n in HG_LOADS}
 
-        def block(tiles, n):
-            return tiles[n // 4][:, n % 4, :]
+        def pair_of(tiles, loads, i):
+            first = max(f for f, n in loads if f <= i)
+            return tiles[first][:, i - first, :]
 
         w2_in = sb([P, 2 * HID], U8, "w2_in")
         w2_perm = sb([P, 2 * HID], U8, "w2_perm")
@@ -60,12 +68,15 @@ def tile_gin_pc_w4_kernel(
         wo = sb([P, 3, 2 * CLS], U8, "wo")
         wos = sb([P, 3, CLS], U8, "wos")
         ident = sb([P, P], F32, "ident")
-        scale_all = sb([P, 2, HID], F32, "scale_all")
-        bo_all = sb([P, CLS], BF16, "bo_all")
-        u_val = [sb([P, 2, HID], BF16, f"u_val{i}") for i in range(NP)]
+        scale_all = sb([P, HID], F32, "scale_all")
+        ones = sb([P, TERMS], F32, "ones")
+        count = sb([P, TERMS], F32, "count")
+        node_t = sb([P, TERMS], F32, "node_t")
+        node_x = sb([P, TERMS], F32, "node_x")
+        node_neg = sb([P, TERMS], F32, "node_neg")
+        u_val = [sb([P, HID], BF16, f"u_val{n}") for n in range(NB)]
         u_grp = [sb([P, 256, 4], BF16, f"u_grp{i}") for i in range(NP)]
         hg_grp = [sb([P, 2, 256, 4], BF16, f"hg_grp{i}") for i in range(NP)]
-        h2_flat = [sb([P, 4, 256], BF16, f"h2_flat{i}") for i in range(NP)]
         h2_grp = [sb([P, 256, 4], BF16, f"h2_grp{i}") for i in range(NP)]
         u_codes = [sb([P, 256], U32, f"u_codes{i}") for i in range(NP)]
         u_scl = [sb([P, 256], U8, f"u_scl{i}") for i in range(NP)]
@@ -73,67 +84,88 @@ def tile_gin_pc_w4_kernel(
         hg_scl = [sb([P, 512], U8, f"hg_scl{i}") for i in range(NP)]
         h2_codes = [sb([P, 256], U32, f"h2_codes{i}") for i in range(NP)]
         h2_scl = [sb([P, 256], U8, f"h2_scl{i}") for i in range(NP)]
-        logits = [sb([P, 2, CLS], F32, f"logits{i}") for i in range(NP)]
-        junk = sb([P, CLS], F32, "junk")
+        h2_flat = [sb([P, 4, 256], BF16, f"h2_flat{i}") for i in range(NP)]
+        bo_pairs = sb([P, 2], BF16, "bo_pairs")
+        bo_all = sb([P, CLS], BF16, "bo_all")
+        lt_sb = [sb([P, 2, 256], F32, f"lt_sb{i}") for i in range(NP)]
+        terms = [sb([P, TERMS], F32, f"terms{n}") for n in range(NB)]
         nmax = sb([P, NB], F32, "nmax")
         ssum = sb([P, NB], F32, "ssum")
-        lns = sb([P, NB], F32, "lns")
+        tsum = sb([P, NB], F32, "tsum")
+        shift = sb([P, NB], F32, "shift")
         res = [sb([P, 2, CLS], F32, f"res{i}") for i in range(NP)]
-        warm = sb([P, 1], F32, "warm")
 
-        u_hbm = u1_bytes.rearrange("(p b) k -> p b k", b=NB)
-        h_hbm = h.rearrange("(p b) k -> p b k", b=NB)
-        g_hbm = h1.rearrange("(p b) k -> p b k", b=NB)
+        u_hbm = u1_bytes.rearrange("(p i b) k -> p i (b k)", i=NP, b=2)
+        h_hbm = h.rearrange("(p i b) k -> p i (b k)", i=NP, b=2)
+        g_hbm = h1.rearrange("(p i b) k -> p i (b k)", i=NP, b=2)
         o_hbm = out.rearrange("(p b) c -> p b c", b=NB)
 
         def load_u(i):
-            nc.sync.dma_start(out=u_raw[i][:], in_=u_hbm[:, 4 * i : 4 * i + 4, :])
+            nc.sync.dma_start(out=u_raw[i][:], in_=u_hbm[:, i : i + dict(U_LOADS)[i], :])
 
         def load_h(i):
-            nc.sync.dma_start(out=h_sb[i][:], in_=h_hbm[:, 4 * i : 4 * i + 4, :])
+            nc.sync.dma_start(out=h_sb[i][:], in_=h_hbm[:, i : i + dict(HG_LOADS)[i], :].bitcast(F32))
 
         def load_g(i):
-            nc.sync.dma_start(out=g_sb[i][:], in_=g_hbm[:, 4 * i : 4 * i + 4, :])
+            nc.sync.dma_start(out=g_sb[i][:], in_=g_hbm[:, i : i + dict(HG_LOADS)[i], :].bitcast(F32))
+
+        def load_w2_scales():
+            w2s_hbm = w2_scales[0].rearrange("(q r) n -> r q n", r=4)
+            for r in range(4):
+                nc.sync.dma_start(out=w2s_in[r:P:32, :].bitcast(I32), in_=w2s_hbm[r].bitcast(I32))
+
+        def load_wo_scales():
+            wos_hbm = wo_scales.rearrange("g (q r) n -> r q g n", r=4)
+            for r in range(4):
+                nc.sync.dma_start(out=wos[r:P:32, :, :].bitcast(I32), in_=wos_hbm[r].bitcast(I32))
 
         make_identity(nc, ident[:])
-        nc.vector.memset(warm[:], 0.0)
         nc.vector.memset(w2s_in[:].bitcast(I32), 0)
         nc.vector.memset(wos[:].rearrange("p g n -> p (g n)").bitcast(I32), 0)
 
-        nc.sync.dma_start(out=w2_in[:], in_=w2_words[0])
         nc.sync.dma_start(out=scale_col[:], in_=u1_scale.rearrange("o (p j) -> p (o j)", j=4))
-        w2s_hbm = w2_scales[0].rearrange("(q r) n -> r q n", r=4)
-        for r in range(4):
-            nc.sync.dma_start(out=w2s_in[r:P:32, :].bitcast(I32), in_=w2s_hbm[r].bitcast(I32))
-        load_u(0)
+        nc.sync.dma_start(out=w2_in[:], in_=w2_words[0])
         load_h(0)
         load_g(0)
-        load_u(1)
-        nc.sync.dma_start(out=b2_col[:], in_=b2_1.rearrange("(p t) -> p t", t=4))
+        load_u(0)
         load_h(1)
+        load_u(1)
         load_g(1)
+        load_u(2)
+        load_w2_scales()
+        load_h(2)
+        nc.sync.dma_start(out=b2_col[:], in_=b2_1.rearrange("(p t) -> p t", t=4))
+        load_g(2)
         nc.sync.dma_start(out=wo[:], in_=wo_words.rearrange("g p n -> p g n"))
-        nc.sync.dma_start(out=bo_col[:], in_=b_out.rearrange("(p t) -> p t", t=2))
-        wos_hbm = wo_scales.rearrange("g (q r) n -> r q g n", r=4)
-        for r in range(4):
-            nc.sync.dma_start(out=wos[r:P:32, :, :].bitcast(I32), in_=wos_hbm[r].bitcast(I32))
+        nc.sync.dma_start(out=bo_pairs[:], in_=b_out.rearrange("(p t) -> p t", t=2))
+        load_h(3)
+        load_g(3)
+        load_wo_scales()
 
-        nc.scalar.activation(out=warm[:], in_=warm[:], func=EXP)
+        banks = {}
 
-        def spread_scale():
+        def make_nodes():
+            nc.vector.memset(ones[:], 1.0)
+            nc.vector.tensor_tensor_scan(out=count[:], data0=ones[:], data1=ones[:], initial=-1.0, op0=MULT, op1=ADD)
+            nc.vector.tensor_scalar(
+                out=node_t[:, 1:], in0=count[:, 1:], scalar1=STEP, scalar2=T0, op0=MULT, op1=ADD
+            )
+            nc.vector.tensor_scalar(
+                out=node_t[:, 0:1], in0=ones[:, 0:1], scalar1=T_TAIL, scalar2=None, op0=MULT
+            )
+            nc.scalar.activation(out=node_x[:], in_=node_t[:], func=EXP)
+            nc.vector.tensor_scalar(out=node_neg[:], in0=node_x[:], scalar1=-1.0, scalar2=None, op0=MULT)
+
+        def turn_scale():
             bank = tr_pool.tile([P, 4, P], F32, name="bank", tag="tr")
+            banks["scale"] = bank
             for j in range(4):
                 nc.tensor.transpose(bank[:, j, :], scale_col[:, j : j + 1].to_broadcast([P, P]), ident[:])
-            for c in range(2):
-                nc.scalar.copy(
-                    out=scale_all[:, c, :].rearrange("p (n j) -> p n j", j=4),
-                    in_=bank[:].rearrange("p j n -> p n j"),
-                )
 
-        def spread_b_out():
-            bank = tr_pool.tile([P, P], F32, name="bank", tag="tr")
-            nc.tensor.transpose(bank[:], bo_col[:].bitcast(F32).to_broadcast([P, P]), ident[:])
-            nc.scalar.copy(out=bo_all[:].bitcast(F32), in_=bank[:])
+        def spread_scale():
+            nc.scalar.copy(
+                out=scale_all[:].rearrange("p (n j) -> p n j", j=4), in_=banks["scale"][:].rearrange("p j n -> p n j")
+            )
 
         def permute_w2_words():
             nc.vector.tensor_copy(
@@ -147,34 +179,25 @@ def tile_gin_pc_w4_kernel(
                 in_=w2s_in[:].rearrange("p (m t) -> p t m", t=4),
             )
 
+
         def widen(i, b):
             nc.vector.tensor_tensor(
-                out=u_val[i][:, b, :], in0=block(u_raw, 2 * i + b).bitcast(FP8), in1=scale_all[:, 0, :], op=MULT
-            )
-
-        def widen_pair(i):
-            c, b0 = i // 2, 2 * (i % 2)
-            nc.vector.tensor_tensor(
-                out=u_val[i][:].rearrange("p b k -> p (b k)"),
-                in0=u_raw[c][:, b0 : b0 + 2, :].rearrange("p b k -> p (b k)").bitcast(FP8),
-                in1=scale_all[:].rearrange("p b k -> p (b k)"),
+                out=u_val[2 * i + b][:],
+                in0=pair_of(u_raw, U_LOADS, i)[:, b * HID : (b + 1) * HID].bitcast(FP8),
+                in1=scale_all[:],
                 op=MULT,
             )
-
-        banks = {}
-
-        def source(x, i, b):
-            if x == "u":
-                return u_val[i][:, b, :]
-            return block(h_sb if x == "h" else g_sb, 2 * i + b)
 
         def turn(x, i):
             bank = tr_pool.tile([P, 2, 2, P], F32, name="bank", tag="tr")
             banks[x, i] = bank
             for b in range(2):
-                words = source(x, i, b).bitcast(F32)
+                if x == "u":
+                    words = u_val[2 * i + b][:].bitcast(F32)
+                else:
+                    words = pair_of(h_sb if x == "h" else g_sb, HG_LOADS, i)[:, b * 256 : (b + 1) * 256]
                 for e in range(2):
-                    nc.tensor.transpose(bank[:, b, e, :], words[:, e : HID // 2 : 2], ident[:])
+                    nc.tensor.transpose(bank[:, b, e, :], words[:, e:256:2], ident[:])
 
         def group(x, i):
             dst = u_grp[i][:] if x == "u" else hg_grp[i][:, 0 if x == "h" else 1]
@@ -195,29 +218,6 @@ def tile_gin_pc_w4_kernel(
         def quantize_h2(i):
             quantize(h2_codes[i], h2_scl[i], h2_grp[i][:].rearrange("p n t -> p (n t)"))
 
-        def matmul_h2(i, b):
-            bank = h2_pool.tile([P, 4, P], F32, name="h2_bank", tag="h2")
-            banks["h2", i, b] = bank
-            nodes = slice(b * P, (b + 1) * P)
-            for t in range(4):
-                nc.tensor.matmul_mx(
-                    out=bank[:, t, :],
-                    lhsT=w2_perm[:, 2 * P * t : 2 * P * (t + 1)].bitcast(FP4X4),
-                    lhsT_scale=w2s_perm[:, P * t : P * (t + 1)],
-                    rhs=u_codes[i][:, nodes].bitcast(FP8X4),
-                    rhs_scale=u_scl[i][:, nodes],
-                    start=True,
-                    stop=True,
-                )
-
-        def bias_h2(i, b):
-            nc.vector.tensor_tensor(
-                out=h2_grp[i][:, b * P : (b + 1) * P, :],
-                in0=banks["h2", i, b][:].rearrange("p t n -> p n t"),
-                in1=b2_col[:].unsqueeze(1).to_broadcast([P, P, 4]),
-                op=ADD,
-            )
-
         def matmul_h2_pair(i):
             for u in range(2):
                 bank = h2_pool.tile([P, 2, 256], F32, name="h2_bank", tag="h2")
@@ -234,180 +234,240 @@ def tile_gin_pc_w4_kernel(
                         stop=True,
                     )
 
-        def bias_h2_scalar(i):
-            for t in range(4):
+        def bias_h2_planes(i, u):
+            for v in range(2):
+                t = 2 * u + v
                 nc.scalar.activation(
-                    out=h2_flat[i][:, t, :],
-                    in_=banks["h2", i, t // 2][:, t % 2, :],
-                    func=IDENT,
-                    bias=b2_col[:, t : t + 1],
+                    out=h2_flat[i][:, t, :], in_=banks["h2", i, u][:, v, :], func=IDENT, bias=b2_col[:, t : t + 1]
                 )
 
         def interleave_h2(i):
             nc.vector.tensor_copy(out=h2_grp[i][:], in_=h2_flat[i][:].rearrange("p t n -> p n t"))
 
-        def cat_codes(i, g, b):
-            n0 = (g * 256 if g < 2 else 0) + b * P
-            codes, scl = (hg_codes[i], hg_scl[i]) if g < 2 else (h2_codes[i], h2_scl[i])
-            return codes[:, n0 : n0 + P].bitcast(FP8X4), scl[:, n0 : n0 + P]
+        def turn_b_out():
+            bank = tr_pool.tile([P, P], F32, name="bank", tag="tr")
+            banks["b_out"] = bank
+            nc.tensor.transpose(bank[:], bo_pairs[:].bitcast(F32).to_broadcast([P, P]), ident[:])
 
-        def wo_codes(g, c):
-            return wo[:, g, 2 * P * c : 2 * P * (c + 1)].bitcast(FP4X4), wos[:, g, c * P : (c + 1) * P]
+        def spread_b_out():
+            nc.scalar.copy(out=bo_all[:].bitcast(F32), in_=banks["b_out"][:])
 
-        def matmul_out(i):
-            bank = lg_pool.tile([P, 2, CLS], F32, name="lg_bank", tag="lg")
-            banks["lg", i] = bank
-            for b in range(2):
-                for c in range(2):
-                    for g in range(3):
-                        x, xs = cat_codes(i, g, b)
-                        w, ws = wo_codes(g, c)
-                        nc.tensor.matmul_mx(
-                            out=bank[:, b, c * P : (c + 1) * P],
-                            lhsT=x, lhsT_scale=xs, rhs=w, rhs_scale=ws,
-                            start=(g == 0), stop=(g == 2),
-                        )
+        def quantize_h2_block(i, b):
+            nodes = slice(b * P, (b + 1) * P)
+            quantize(h2_codes[i][:, nodes], h2_scl[i][:, nodes], h2_grp[i][:, nodes, :].rearrange("p n t -> p (n t)"))
 
-        def bias_out(i, blocks=BOTH):
+        def matmul_rows(i, b, groups):
+            if groups[0] == 0:
+                banks["rows", i, b] = tr_pool.tile([P, CLS], F32, name="bank", tag="tr")
+            for g in groups:
+                codes, scl = (hg_codes[i], hg_scl[i]) if g < 2 else (h2_codes[i], h2_scl[i])
+                nodes = slice(256 * (g % 2) * (g < 2) + b * P, 256 * (g % 2) * (g < 2) + (b + 1) * P)
+                nc.tensor.matmul_mx(
+                    out=banks["rows", i, b][:],
+                    lhsT=codes[:, nodes].bitcast(FP8X4),
+                    lhsT_scale=scl[:, nodes],
+                    rhs=wo[:, g, :].bitcast(FP4X4),
+                    rhs_scale=wos[:, g, :],
+                    start=(g == 0),
+                    stop=(g == 2),
+                )
+
+        def matmul_pair_rows(i, groups):
+            if groups[0] == 0:
+                banks["rows", i] = lg_pool.tile([P, 2, CLS], F32, name="lg_bank", tag="lg")
+            for g in groups:
+                codes, scl = (hg_codes[i], hg_scl[i]) if g < 2 else (h2_codes[i], h2_scl[i])
+                for b in range(2):
+                    nodes = slice(256 * (g % 2) + b * P, 256 * (g % 2) + (b + 1) * P)
+                    nc.tensor.matmul_mx(
+                        out=banks["rows", i][:, b, :],
+                        lhsT=codes[:, nodes].bitcast(FP8X4),
+                        lhsT_scale=scl[:, nodes],
+                        rhs=wo[:, g, :].bitcast(FP4X4),
+                        rhs_scale=wos[:, g, :],
+                        start=(g == 0 and b == 0),
+                        stop=(g == 2 and b == 1),
+                    )
+
+        def bias_pair(i):
             nc.vector.tensor_tensor(
-                out=logits[i][:, blocks, :],
-                in0=banks["lg", i][:, blocks, :],
-                in1=bo_all[:].unsqueeze(1).to_broadcast([P, blocks.stop - blocks.start, CLS]),
-                op=ADD,
+                out=lt_sb[i][:], in0=banks["rows", i][:], in1=bo_all[:].unsqueeze(1).to_broadcast([P, 2, CLS]), op=ADD
             )
 
-        def row_max(i, blocks=BOTH):
-            nc.vector.tensor_reduce(
-                out=nmax[:, 2 * i + blocks.start : 2 * i + blocks.stop],
-                in_=logits[i][:, blocks, :],
-                axis=AX,
-                op=MAX,
-                negate=True,
-            )
+        def max_pair(i):
+            nc.vector.tensor_reduce(out=nmax[:, 2 * i : 2 * i + 2], in_=lt_sb[i][:], axis=AX, op=MAX, negate=True)
 
-        def exp_sum(i, b):
+        def finish_rows_scalar(i, b):
+            n = 2 * i + b
+            nc.scalar.activation(out=res[i][:, b, :], in_=lt_sb[i][:, b, :], func=IDENT, bias=shift[:, n : n + 1])
+
+        def bias_rows(i, b):
+            nc.vector.tensor_tensor(out=lt_sb[i][:, b, :], in0=banks["rows", i, b][:], in1=bo_all[:], op=ADD)
+
+        def max_rows(i, b):
+            n = 2 * i + b
+            nc.vector.tensor_reduce(out=nmax[:, n : n + 1], in_=lt_sb[i][:, b, :], axis=AX, op=MAX, negate=True)
+
+        def exp_rows(i, b):
             n = 2 * i + b
             nc.scalar.activation(
-                out=junk[:],
-                in_=logits[i][:, b, :],
+                out=res[i][:, b, :],
+                in_=lt_sb[i][:, b, :],
                 func=EXP,
                 bias=nmax[:, n : n + 1],
                 accum_out=ssum[:, n : n + 1],
             )
 
-        def log_sum(b0, b1):
-            nc.scalar.activation(out=lns[:, b0:b1], in_=ssum[:, b0:b1], func=LN)
+        def offset_max(n0, n1):
+            nc.vector.tensor_scalar(
+                out=shift[:, n0:n1], in0=nmax[:, n0:n1], scalar1=-LOG_CONST, scalar2=None, op0=ADD
+            )
 
-        def finish(i, b):
+        def finish_rows(i, b):
             n = 2 * i + b
             nc.vector.tensor_scalar(
                 out=res[i][:, b, :],
-                in0=logits[i][:, b, :],
-                scalar1=nmax[:, n : n + 1],
-                scalar2=lns[:, n : n + 1],
+                in0=lt_sb[i][:, b, :],
+                scalar1=shift[:, n : n + 1],
+                scalar2=tsum[:, n : n + 1],
                 op0=ADD,
-                op1=SUB,
+                op1=ADD,
             )
 
-        def store(i, b):
-            nc.sync.dma_start(out=o_hbm[:, 2 * i + b, :], in_=res[i][:, b, :])
+        def log_terms(i, b):
+            n = 2 * i + b
+            nc.scalar.activation(
+                out=terms[n][:],
+                in_=node_neg[:],
+                func=EXP,
+                scale=ssum[:, n : n + 1],
+                bias=LOG_STEP,
+                accum_out=tsum[:, n : n + 1],
+            )
 
-        permute_w2_words()
+        def make_shift(i):
+            cols = slice(2 * i, 2 * i + 2)
+            nc.vector.scalar_tensor_tensor(
+                out=shift[:, cols], in0=tsum[:, cols], scalar=-LOG_CONST, in1=nmax[:, cols], op0=ADD, op1=ADD
+            )
+
+        def store(i, b0, b1):
+            nc.sync.dma_start(out=o_hbm[:, 2 * i + b0 : 2 * i + b1, :], in_=res[i][:, b0:b1, :])
+
+        make_nodes()
+        turn_scale()
         spread_scale()
         turn("h", 0)
-        permute_w2_scales()
+        group("h", 0)
+        permute_w2_words()
+        turn("g", 0)
+        group("g", 0)
         widen(0, 0)
         widen(0, 1)
-        group("h", 0)
-        widen_pair(1)
         turn("h", 1)
         group("h", 1)
+        widen(1, 0)
+        widen(1, 1)
         turn("u", 0)
-        widen_pair(2)
-        turn("g", 0)
-        turn("u", 1)
         group("u", 0)
-        turn("g", 1)
-        turn("u", 2)
-        group("u", 1)
-        quantize_u(0)
-        widen_pair(3)
-        group("g", 1)
-        quantize_u(1)
-        matmul_h2(0, 1)
-        group("g", 0)
-        matmul_h2(0, 0)
-        spread_b_out()
-        bias_h2(0, 0)
-        bias_h2(0, 1)
-        group("u", 2)
         quantize_hg(0)
+        turn("g", 1)
+        group("g", 1)
+        quantize_u(0)
+        turn("u", 1)
+        group("u", 1)
+        permute_w2_scales()
         turn("h", 2)
         group("h", 2)
+        widen(2, 0)
+        widen(2, 1)
+        matmul_h2_pair(0)
+        bias_h2_planes(0, 0)
+        bias_h2_planes(0, 1)
+        quantize_u(1)
+        turn("u", 2)
+        group("u", 2)
+        widen(3, 0)
+        widen(3, 1)
+        matmul_h2_pair(1)
+        bias_h2_planes(1, 0)
+        bias_h2_planes(1, 1)
+        quantize_hg(1)
         turn("u", 3)
         group("u", 3)
-        quantize_h2(0)
-        quantize_u(3)
-        matmul_h2_pair(1)
-        quantize_u(2)
-        bias_h2_scalar(1)
-        matmul_out(0)
-        quantize_hg(1)
+        interleave_h2(0)
         turn("g", 2)
         group("g", 2)
-        interleave_h2(1)
-        bias_out(0, slice(0, 2))
-        quantize_h2(1)
-        row_max(0, slice(0, 2))
+        quantize_u(2)
+        turn_b_out()
+        spread_b_out()
+        quantize_h2(0)
         matmul_h2_pair(2)
-        bias_h2_scalar(2)
-        quantize_hg(2)
-        matmul_out(1)
-        bias_out(1, slice(0, 2))
-        turn("g", 3)
+        bias_h2_planes(2, 0)
+        bias_h2_planes(2, 1)
+        interleave_h2(1)
+        matmul_pair_rows(0, (0, 1, 2))
+        quantize_u(3)
         turn("h", 3)
-        interleave_h2(2)
-        row_max(1, slice(0, 2))
-        exp_sum(0, 0)
-        exp_sum(0, 1)
-        quantize_h2(2)
-        matmul_h2(3, 0)
-        group("g", 3)
         group("h", 3)
-        matmul_h2(3, 1)
-        matmul_out(2)
-        bias_h2(3, 0)
-        bias_h2(3, 1)
+        quantize_h2(1)
+        turn("g", 3)
+        group("g", 3)
+        quantize_hg(2)
+        matmul_h2_pair(3)
+        bias_h2_planes(3, 0)
+        bias_h2_planes(3, 1)
+        bias_pair(0)
+        matmul_pair_rows(1, (0, 1, 2))
+        interleave_h2(2)
+        max_pair(0)
+        exp_rows(0, 0)
+        exp_rows(0, 1)
+        quantize_h2(2)
+        matmul_pair_rows(2, (0, 1, 2))
+        log_terms(0, 0)
+        log_terms(0, 1)
+        bias_pair(1)
         quantize_hg(3)
-        quantize_h2(3)
-        bias_out(2, slice(0, 2))
-        exp_sum(1, 0)
-        exp_sum(1, 1)
-        matmul_out(3)
-        bias_out(3, slice(0, 1))
-        row_max(2, slice(0, 2))
-        log_sum(0, 4)
-        exp_sum(2, 0)
-        exp_sum(2, 1)
-        row_max(3, slice(0, 1))
-        exp_sum(3, 0)
-        bias_out(3, slice(1, 2))
-        row_max(3, slice(1, 2))
-        exp_sum(3, 1)
-        finish(0, 0)
-        finish(0, 1)
-        store(0, 0)
-        finish(1, 0)
-        finish(1, 1)
-        store(1, 1)
-        store(0, 1)
-        store(1, 0)
-        log_sum(4, 8)
-        finish(3, 0)
-        finish(2, 1)
-        store(3, 0)
-        finish(2, 0)
-        store(2, 1)
-        store(2, 0)
-        finish(3, 1)
-        store(3, 1)
+        matmul_rows(3, 0, (0, 1))
+        max_pair(1)
+        matmul_rows(3, 1, (0, 1))
+        exp_rows(1, 0)
+        exp_rows(1, 1)
+        interleave_h2(3)
+        log_terms(1, 0)
+        log_terms(1, 1)
+        make_shift(0)
+        finish_rows_scalar(0, 0)
+        finish_rows_scalar(0, 1)
+        quantize_h2_block(3, 0)
+        store(0, 0, 2)
+        matmul_rows(3, 0, (2,))
+        quantize_h2_block(3, 1)
+        matmul_rows(3, 1, (2,))
+        bias_pair(2)
+        make_shift(1)
+        finish_rows_scalar(1, 0)
+        finish_rows_scalar(1, 1)
+        bias_rows(3, 0)
+        store(1, 0, 2)
+        max_pair(2)
+        exp_rows(2, 0)
+        exp_rows(2, 1)
+        bias_rows(3, 1)
+        log_terms(2, 0)
+        log_terms(2, 1)
+        max_rows(3, 0)
+        exp_rows(3, 0)
+        max_rows(3, 1)
+        exp_rows(3, 1)
+        offset_max(4, 8)
+        log_terms(3, 0)
+        log_terms(3, 1)
+        finish_rows(2, 0)
+        finish_rows(2, 1)
+        store(2, 0, 2)
+        finish_rows(3, 0)
+        store(3, 0, 1)
+        finish_rows(3, 1)
+        store(3, 1, 2)

@@ -34,7 +34,8 @@ T_TAIL = T0 + STEP - math.log(math.exp(STEP) - 1.0)
 LOG_CONST = STEP * (math.exp(-math.exp(T_TAIL)) + sum(math.exp(-math.exp(T0 + j * STEP)) for j in range(1, TERMS)))
 
 U_LOADS = ((0, 1), (1, 1), (2, 2))
-HG_LOADS = ((0, 1), (1, 1), (2, 1), (3, 1))
+H_LOADS = ((0, 1), (1, 1), (2, 1), (3, 1))
+G_LOADS = ((0, 1), (1, 1), (2, 1), (3, 1))
 
 
 def tile_gin_pc_w4_kernel(
@@ -43,19 +44,20 @@ def tile_gin_pc_w4_kernel(
     nc = tc.nc
     with ExitStack() as ctx:
         keep = ctx.enter_context(tc.tile_pool(name="keep", bufs=1))
-        tr_pool = ctx.enter_context(tc.psum_pool(name="tr_pool", bufs=4))
-        h2_pool = ctx.enter_context(tc.psum_pool(name="h2_pool", bufs=2))
-        lg_pool = ctx.enter_context(tc.psum_pool(name="lg_pool", bufs=2))
+        psum = ctx.enter_context(tc.psum_pool(name="psum", bufs=1))
         ctx.enter_context(tc.manual_schedule())
 
         def sb(shape, dtype, name):
             return keep.tile(shape, dtype, name=name, align_bytes=64)
 
+        def take_bank(k, shape):
+            return psum.tile(shape, F32, name=f"bank{k}", tag=f"bank{k}")
+
         scale_col = sb([P, 4], F32, "scale_col")
         b2_col = sb([P, 4], BF16, "b2_col")
         u_raw = {i: sb([P, n, 2 * HID], U8, f"u_raw{i}") for i, n in U_LOADS}
-        h_sb = {i: sb([P, n, HID], F32, f"h_sb{i}") for i, n in HG_LOADS}
-        g_sb = {i: sb([P, n, HID], F32, f"g_sb{i}") for i, n in HG_LOADS}
+        h_sb = {i: sb([P, n, HID], F32, f"h_sb{i}") for i, n in H_LOADS}
+        g_sb = {i: sb([P, n, HID], F32, f"g_sb{i}") for i, n in G_LOADS}
 
         def pair_of(tiles, loads, i):
             first = max(f for f, n in loads if f <= i)
@@ -85,7 +87,6 @@ def tile_gin_pc_w4_kernel(
         h2_codes = [sb([P, 256], U32, f"h2_codes{i}") for i in range(NP)]
         h2_scl = [sb([P, 256], U8, f"h2_scl{i}") for i in range(NP)]
         h2_flat = [sb([P, 4, 256], BF16, f"h2_flat{i}") for i in range(NP)]
-        bo_pairs = sb([P, 2], BF16, "bo_pairs")
         bo_all = sb([P, CLS], BF16, "bo_all")
         lt_sb = [sb([P, 2, 256], F32, f"lt_sb{i}") for i in range(NP)]
         terms = [sb([P, TERMS], F32, f"terms{n}") for n in range(NB)]
@@ -104,10 +105,10 @@ def tile_gin_pc_w4_kernel(
             nc.sync.dma_start(out=u_raw[i][:], in_=u_hbm[:, i : i + dict(U_LOADS)[i], :])
 
         def load_h(i):
-            nc.sync.dma_start(out=h_sb[i][:], in_=h_hbm[:, i : i + dict(HG_LOADS)[i], :].bitcast(F32))
+            nc.sync.dma_start(out=h_sb[i][:], in_=h_hbm[:, i : i + dict(H_LOADS)[i], :].bitcast(F32))
 
         def load_g(i):
-            nc.sync.dma_start(out=g_sb[i][:], in_=g_hbm[:, i : i + dict(HG_LOADS)[i], :].bitcast(F32))
+            nc.sync.dma_start(out=g_sb[i][:], in_=g_hbm[:, i : i + dict(G_LOADS)[i], :].bitcast(F32))
 
         def load_w2_scales():
             w2s_hbm = w2_scales[0].rearrange("(q r) n -> r q n", r=4)
@@ -131,16 +132,16 @@ def tile_gin_pc_w4_kernel(
         load_h(1)
         load_u(1)
         load_g(1)
-        load_u(2)
         load_w2_scales()
+        load_u(2)
         load_h(2)
         nc.sync.dma_start(out=b2_col[:], in_=b2_1.rearrange("(p t) -> p t", t=4))
         load_g(2)
         nc.sync.dma_start(out=wo[:], in_=wo_words.rearrange("g p n -> p g n"))
-        nc.sync.dma_start(out=bo_pairs[:], in_=b_out.rearrange("(p t) -> p t", t=2))
         load_h(3)
         load_g(3)
         load_wo_scales()
+        nc.sync.dma_start(out=bo_all[:], in_=b_out.partition_broadcast(P))
 
         banks = {}
 
@@ -156,8 +157,8 @@ def tile_gin_pc_w4_kernel(
             nc.scalar.activation(out=node_x[:], in_=node_t[:], func=EXP)
             nc.vector.tensor_scalar(out=node_neg[:], in0=node_x[:], scalar1=-1.0, scalar2=None, op0=MULT)
 
-        def turn_scale():
-            bank = tr_pool.tile([P, 4, P], F32, name="bank", tag="tr")
+        def turn_scale(k):
+            bank = take_bank(k, [P, 4, P])
             banks["scale"] = bank
             for j in range(4):
                 nc.tensor.transpose(bank[:, j, :], scale_col[:, j : j + 1].to_broadcast([P, P]), ident[:])
@@ -188,14 +189,15 @@ def tile_gin_pc_w4_kernel(
                 op=MULT,
             )
 
-        def turn(x, i):
-            bank = tr_pool.tile([P, 2, 2, P], F32, name="bank", tag="tr")
+        def turn(x, i, k):
+            bank = take_bank(k, [P, 2, 2, P])
             banks[x, i] = bank
             for b in range(2):
                 if x == "u":
                     words = u_val[2 * i + b][:].bitcast(F32)
                 else:
-                    words = pair_of(h_sb if x == "h" else g_sb, HG_LOADS, i)[:, b * 256 : (b + 1) * 256]
+                    rows = pair_of(h_sb, H_LOADS, i) if x == "h" else pair_of(g_sb, G_LOADS, i)
+                    words = rows[:, b * 256 : (b + 1) * 256]
                 for e in range(2):
                     nc.tensor.transpose(bank[:, b, e, :], words[:, e:256:2], ident[:])
 
@@ -218,9 +220,9 @@ def tile_gin_pc_w4_kernel(
         def quantize_h2(i):
             quantize(h2_codes[i], h2_scl[i], h2_grp[i][:].rearrange("p n t -> p (n t)"))
 
-        def matmul_h2_pair(i):
+        def matmul_h2_pair(i, k):
             for u in range(2):
-                bank = h2_pool.tile([P, 2, 256], F32, name="h2_bank", tag="h2")
+                bank = take_bank(k[u], [P, 2, 256])
                 banks["h2", i, u] = bank
                 for v in range(2):
                     t = 2 * u + v
@@ -244,21 +246,13 @@ def tile_gin_pc_w4_kernel(
         def interleave_h2(i):
             nc.vector.tensor_copy(out=h2_grp[i][:], in_=h2_flat[i][:].rearrange("p t n -> p n t"))
 
-        def turn_b_out():
-            bank = tr_pool.tile([P, P], F32, name="bank", tag="tr")
-            banks["b_out"] = bank
-            nc.tensor.transpose(bank[:], bo_pairs[:].bitcast(F32).to_broadcast([P, P]), ident[:])
-
-        def spread_b_out():
-            nc.scalar.copy(out=bo_all[:].bitcast(F32), in_=banks["b_out"][:])
-
         def quantize_h2_block(i, b):
             nodes = slice(b * P, (b + 1) * P)
             quantize(h2_codes[i][:, nodes], h2_scl[i][:, nodes], h2_grp[i][:, nodes, :].rearrange("p n t -> p (n t)"))
 
-        def matmul_rows(i, b, groups):
+        def matmul_rows(i, b, groups, k=None):
             if groups[0] == 0:
-                banks["rows", i, b] = tr_pool.tile([P, CLS], F32, name="bank", tag="tr")
+                banks["rows", i, b] = take_bank(k, [P, CLS])
             for g in groups:
                 codes, scl = (hg_codes[i], hg_scl[i]) if g < 2 else (h2_codes[i], h2_scl[i])
                 nodes = slice(256 * (g % 2) * (g < 2) + b * P, 256 * (g % 2) * (g < 2) + (b + 1) * P)
@@ -272,9 +266,9 @@ def tile_gin_pc_w4_kernel(
                     stop=(g == 2),
                 )
 
-        def matmul_pair_rows(i, groups):
+        def matmul_pair_rows(i, groups, k=None):
             if groups[0] == 0:
-                banks["rows", i] = lg_pool.tile([P, 2, CLS], F32, name="lg_bank", tag="lg")
+                banks["rows", i] = take_bank(k, [P, 2, CLS])
             for g in groups:
                 codes, scl = (hg_codes[i], hg_scl[i]) if g < 2 else (h2_codes[i], h2_scl[i])
                 for b in range(2):
@@ -355,115 +349,113 @@ def tile_gin_pc_w4_kernel(
             nc.sync.dma_start(out=o_hbm[:, 2 * i + b0 : 2 * i + b1, :], in_=res[i][:, b0:b1, :])
 
         make_nodes()
-        turn_scale()
+        turn_scale(0)
         spread_scale()
-        turn("h", 0)
+        turn("h", 0, 1)
         group("h", 0)
         permute_w2_words()
-        turn("g", 0)
+        turn("g", 0, 2)
         group("g", 0)
         widen(0, 0)
         widen(0, 1)
-        turn("h", 1)
+        turn("h", 1, 3)
         group("h", 1)
         widen(1, 0)
         widen(1, 1)
-        turn("u", 0)
+        turn("u", 0, 0)
         group("u", 0)
         quantize_hg(0)
-        turn("g", 1)
+        turn("g", 1, 1)
         group("g", 1)
         quantize_u(0)
-        turn("u", 1)
+        turn("u", 1, 2)
         group("u", 1)
         permute_w2_scales()
-        turn("h", 2)
+        turn("h", 2, 3)
         group("h", 2)
         widen(2, 0)
         widen(2, 1)
-        matmul_h2_pair(0)
+        matmul_h2_pair(0, (4, 5))
         bias_h2_planes(0, 0)
         bias_h2_planes(0, 1)
         quantize_u(1)
-        turn("u", 2)
+        turn("u", 2, 0)
         group("u", 2)
         widen(3, 0)
         widen(3, 1)
-        matmul_h2_pair(1)
+        matmul_h2_pair(1, (4, 5))
         bias_h2_planes(1, 0)
         bias_h2_planes(1, 1)
         quantize_hg(1)
-        turn("u", 3)
+        turn("u", 3, 1)
         group("u", 3)
         interleave_h2(0)
-        turn("g", 2)
+        turn("g", 2, 2)
         group("g", 2)
         quantize_u(2)
-        turn_b_out()
-        spread_b_out()
-        quantize_h2(0)
-        matmul_h2_pair(2)
+        matmul_h2_pair(2, (4, 5))
         bias_h2_planes(2, 0)
         bias_h2_planes(2, 1)
+        quantize_h2(0)
+        matmul_pair_rows(0, (0, 1, 2), 6)
         interleave_h2(1)
-        matmul_pair_rows(0, (0, 1, 2))
-        quantize_u(3)
-        turn("h", 3)
+        turn("h", 3, 0)
         group("h", 3)
-        quantize_h2(1)
-        turn("g", 3)
+        quantize_u(3)
+        turn("g", 3, 1)
         group("g", 3)
-        quantize_hg(2)
-        matmul_h2_pair(3)
+        quantize_h2(1)
+        matmul_h2_pair(3, (4, 5))
         bias_h2_planes(3, 0)
         bias_h2_planes(3, 1)
+        quantize_hg(2)
+        matmul_pair_rows(1, (0, 1, 2), 7)
         bias_pair(0)
-        matmul_pair_rows(1, (0, 1, 2))
         interleave_h2(2)
         max_pair(0)
         exp_rows(0, 0)
         exp_rows(0, 1)
         quantize_h2(2)
-        matmul_pair_rows(2, (0, 1, 2))
+        matmul_pair_rows(2, (0, 1, 2), 6)
         log_terms(0, 0)
         log_terms(0, 1)
-        bias_pair(1)
         quantize_hg(3)
-        matmul_rows(3, 0, (0, 1))
+        matmul_rows(3, 0, (0, 1), 2)
+        bias_pair(1)
+        matmul_rows(3, 1, (0, 1), 3)
+        interleave_h2(3)
         max_pair(1)
-        matmul_rows(3, 1, (0, 1))
         exp_rows(1, 0)
         exp_rows(1, 1)
-        interleave_h2(3)
-        log_terms(1, 0)
-        log_terms(1, 1)
         make_shift(0)
         finish_rows_scalar(0, 0)
-        finish_rows_scalar(0, 1)
-        quantize_h2_block(3, 0)
-        store(0, 0, 2)
-        matmul_rows(3, 0, (2,))
-        quantize_h2_block(3, 1)
-        matmul_rows(3, 1, (2,))
         bias_pair(2)
-        make_shift(1)
-        finish_rows_scalar(1, 0)
-        finish_rows_scalar(1, 1)
-        bias_rows(3, 0)
-        store(1, 0, 2)
+        log_terms(1, 0)
+        log_terms(1, 1)
+        quantize_h2_block(3, 0)
+        matmul_rows(3, 0, (2,))
+        finish_rows_scalar(0, 1)
+        quantize_h2_block(3, 1)
+        store(0, 0, 2)
+        matmul_rows(3, 1, (2,))
         max_pair(2)
         exp_rows(2, 0)
         exp_rows(2, 1)
-        bias_rows(3, 1)
+        offset_max(2, 6)
         log_terms(2, 0)
         log_terms(2, 1)
+        bias_rows(3, 0)
+        bias_rows(3, 1)
         max_rows(3, 0)
         exp_rows(3, 0)
         max_rows(3, 1)
         exp_rows(3, 1)
-        offset_max(4, 8)
+        finish_rows(1, 0)
+        finish_rows(1, 1)
+        store(1, 0, 2)
         log_terms(3, 0)
         log_terms(3, 1)
+        offset_max(6, 8)
         finish_rows(2, 0)
         finish_rows(2, 1)
         store(2, 0, 2)

@@ -70,6 +70,7 @@ def tile_gin_pc_w4_kernel(
         wo = sb([P, 3, 2 * CLS], U8, "wo")
         wos = sb([P, 3, CLS], U8, "wos")
         ident = sb([P, P], F32, "ident")
+        ident_bf = sb([P, P], BF16, "ident_bf")
         scale_all = sb([P, HID], F32, "scale_all")
         ones = sb([P, TERMS], F32, "ones")
         count = sb([P, TERMS], F32, "count")
@@ -246,9 +247,20 @@ def tile_gin_pc_w4_kernel(
         def interleave_h2(i):
             nc.vector.tensor_copy(out=h2_grp[i][:], in_=h2_flat[i][:].rearrange("p t n -> p n t"))
 
-        def quantize_h2_block(i, b):
-            nodes = slice(b * P, (b + 1) * P)
-            quantize(h2_codes[i][:, nodes], h2_scl[i][:, nodes], h2_grp[i][:, nodes, :].rearrange("p n t -> p (n t)"))
+        def make_ident_bf16():
+            nc.vector.tensor_copy(out=ident_bf[:], in_=ident[:])
+
+        def weave_h2(i, k):
+            bank = psum.tile([P, 2, HID], BF16, name=f"bank{k}", tag=f"bank{k}")
+            banks["weave", i] = bank
+            woven = h2_flat[i][:].rearrange("p t n -> p n t")
+            for b in range(2):
+                nc.tensor.matmul(bank[:, b, :], lhsT=ident_bf[:], rhs=woven[:, b * P : (b + 1) * P, :], start=True, stop=True)
+
+        def copy_weave(i):
+            nc.scalar.copy(
+                out=h2_grp[i][:].rearrange("p n t -> p (n t)"), in_=banks["weave", i][:].rearrange("p b k -> p (b k)")
+            )
 
         def matmul_rows(i, b, groups, k=None):
             if groups[0] == 0:
@@ -353,45 +365,46 @@ def tile_gin_pc_w4_kernel(
         spread_scale()
         turn("h", 0, 1)
         group("h", 0)
-        permute_w2_words()
+        make_ident_bf16()
         turn("g", 0, 2)
         group("g", 0)
-        widen(0, 0)
-        widen(0, 1)
+        permute_w2_words()
         turn("h", 1, 3)
         group("h", 1)
-        widen(1, 0)
-        widen(1, 1)
+        widen(0, 0)
+        widen(0, 1)
         turn("u", 0, 0)
         group("u", 0)
-        quantize_hg(0)
+        widen(1, 0)
+        widen(1, 1)
         turn("g", 1, 1)
         group("g", 1)
-        quantize_u(0)
+        quantize_hg(0)
         turn("u", 1, 2)
         group("u", 1)
-        permute_w2_scales()
+        quantize_u(0)
         turn("h", 2, 3)
         group("h", 2)
-        widen(2, 0)
-        widen(2, 1)
+        permute_w2_scales()
         matmul_h2_pair(0, (4, 5))
         bias_h2_planes(0, 0)
         bias_h2_planes(0, 1)
-        quantize_u(1)
+        widen(2, 0)
+        widen(2, 1)
         turn("u", 2, 0)
         group("u", 2)
-        widen(3, 0)
-        widen(3, 1)
+        quantize_u(1)
         matmul_h2_pair(1, (4, 5))
         bias_h2_planes(1, 0)
         bias_h2_planes(1, 1)
-        quantize_hg(1)
+        widen(3, 0)
+        widen(3, 1)
         turn("u", 3, 1)
         group("u", 3)
-        interleave_h2(0)
+        quantize_hg(1)
         turn("g", 2, 2)
         group("g", 2)
+        interleave_h2(0)
         quantize_u(2)
         matmul_h2_pair(2, (4, 5))
         bias_h2_planes(2, 0)
@@ -399,53 +412,53 @@ def tile_gin_pc_w4_kernel(
         quantize_h2(0)
         matmul_pair_rows(0, (0, 1, 2), 6)
         interleave_h2(1)
-        turn("h", 3, 0)
-        group("h", 3)
         quantize_u(3)
-        turn("g", 3, 1)
-        group("g", 3)
-        quantize_h2(1)
-        matmul_h2_pair(3, (4, 5))
+        matmul_h2_pair(3, (0, 1))
         bias_h2_planes(3, 0)
         bias_h2_planes(3, 1)
-        quantize_hg(2)
+        quantize_h2(1)
         matmul_pair_rows(1, (0, 1, 2), 7)
+        quantize_hg(2)
+        turn("h", 3, 2)
+        group("h", 3)
         bias_pair(0)
+        turn("g", 3, 3)
+        group("g", 3)
         interleave_h2(2)
+        weave_h2(3, 4)
+        copy_weave(3)
         max_pair(0)
         exp_rows(0, 0)
         exp_rows(0, 1)
-        quantize_h2(2)
-        matmul_pair_rows(2, (0, 1, 2), 6)
+        bias_pair(1)
         log_terms(0, 0)
         log_terms(0, 1)
-        quantize_hg(3)
-        matmul_rows(3, 0, (0, 1), 2)
-        bias_pair(1)
-        matmul_rows(3, 1, (0, 1), 3)
-        interleave_h2(3)
+        quantize_h2(2)
+        matmul_pair_rows(2, (0, 1, 2), 6)
         max_pair(1)
         exp_rows(1, 0)
         exp_rows(1, 1)
-        make_shift(0)
-        finish_rows_scalar(0, 0)
+        quantize_hg(3)
+        matmul_rows(3, 0, (0, 1), 5)
+        quantize_h2(3)
+        matmul_rows(3, 1, (0, 1), 0)
         bias_pair(2)
+        matmul_rows(3, 0, (2,))
+        make_shift(0)
+        matmul_rows(3, 1, (2,))
+        finish_rows_scalar(0, 0)
+        max_pair(2)
         log_terms(1, 0)
         log_terms(1, 1)
-        quantize_h2_block(3, 0)
-        matmul_rows(3, 0, (2,))
+        bias_rows(3, 0)
         finish_rows_scalar(0, 1)
-        quantize_h2_block(3, 1)
+        bias_rows(3, 1)
         store(0, 0, 2)
-        matmul_rows(3, 1, (2,))
-        max_pair(2)
         exp_rows(2, 0)
         exp_rows(2, 1)
         offset_max(2, 6)
         log_terms(2, 0)
         log_terms(2, 1)
-        bias_rows(3, 0)
-        bias_rows(3, 1)
         max_rows(3, 0)
         exp_rows(3, 0)
         max_rows(3, 1)

@@ -36,6 +36,7 @@ LOG_CONST = STEP * (math.exp(-math.exp(T_TAIL)) + sum(math.exp(-math.exp(T0 + j 
 U_LOADS = ((0, 1), (1, 1), (2, 2))
 H_LOADS = ((0, 1), (1, 1), (2, 1), (3, 1))
 G_LOADS = ((0, 1), (1, 1), (2, 1), (3, 1))
+H2_UNITS = ((0, 1), (1, 1), (2, 1), (3, 1))
 
 
 def tile_gin_pc_w4_kernel(
@@ -78,16 +79,18 @@ def tile_gin_pc_w4_kernel(
         node_x = sb([P, TERMS], F32, "node_x")
         node_neg = sb([P, TERMS], F32, "node_neg")
         u_val = [sb([P, HID], BF16, f"u_val{n}") for n in range(NB)]
-        u_grp = [sb([P, 256, 4], BF16, f"u_grp{i}") for i in range(NP)]
+        u_grp_all = sb([P, 4 * NODES], BF16, "u_grp")
+        u_grp = [u_grp_all[:, 1024 * i : 1024 * (i + 1)].rearrange("p (n t) -> p n t", t=4) for i in range(NP)]
         hg_grp = [sb([P, 2, 256, 4], BF16, f"hg_grp{i}") for i in range(NP)]
         h2_grp = [sb([P, 256, 4], BF16, f"h2_grp{i}") for i in range(NP)]
-        u_codes = [sb([P, 256], U32, f"u_codes{i}") for i in range(NP)]
-        u_scl = [sb([P, 256], U8, f"u_scl{i}") for i in range(NP)]
+        u_codes = sb([P, NODES], U32, "u_codes")
+        u_scl = sb([P, NODES], U8, "u_scl")
         hg_codes = [sb([P, 512], U32, f"hg_codes{i}") for i in range(NP)]
         hg_scl = [sb([P, 512], U8, f"hg_scl{i}") for i in range(NP)]
         h2_codes = [sb([P, 256], U32, f"h2_codes{i}") for i in range(NP)]
         h2_scl = [sb([P, 256], U8, f"h2_scl{i}") for i in range(NP)]
-        h2_flat = [sb([P, 4, 256], BF16, f"h2_flat{i}") for i in range(NP)]
+        planes = {i: sb([P, 4, 256 * n], BF16, f"planes{i}") for i, n in H2_UNITS}
+        h2_flat = [planes[f][:, :, 256 * (i - f) : 256 * (i - f + 1)] for f, n in H2_UNITS for i in range(f, f + n)]
         bo_all = sb([P, CLS], BF16, "bo_all")
         lt_sb = [sb([P, 2, 256], F32, f"lt_sb{i}") for i in range(NP)]
         terms = [sb([P, TERMS], F32, f"terms{n}") for n in range(NB)]
@@ -203,7 +206,7 @@ def tile_gin_pc_w4_kernel(
                     nc.tensor.transpose(bank[:, b, e, :], words[:, e:256:2], ident[:])
 
         def group(x, i):
-            dst = u_grp[i][:] if x == "u" else hg_grp[i][:, 0 if x == "h" else 1]
+            dst = u_grp[i] if x == "u" else hg_grp[i][:, 0 if x == "h" else 1]
             nc.scalar.copy(
                 out=dst.rearrange("p (b n) t -> p b n t", b=2).bitcast(F32),
                 in_=banks[x, i][:].rearrange("p b e n -> p b n e"),
@@ -213,7 +216,8 @@ def tile_gin_pc_w4_kernel(
             nc.vector.quantize_mx(out=codes[:].bitcast(FP8X4), scales=scl[:], in_=grp)
 
         def quantize_u(i):
-            quantize(u_codes[i], u_scl[i], u_grp[i][:].rearrange("p n t -> p (n t)"))
+            nodes = slice(256 * i, 256 * (i + 1))
+            quantize(u_codes[:, nodes], u_scl[:, nodes], u_grp_all[:, 1024 * i : 1024 * (i + 1)])
 
         def quantize_hg(i):
             quantize(hg_codes[i], hg_scl[i], hg_grp[i][:].rearrange("p s n t -> p (s n t)"))
@@ -231,8 +235,8 @@ def tile_gin_pc_w4_kernel(
                         out=bank[:, v, :],
                         lhsT=w2_perm[:, 2 * P * t : 2 * P * (t + 1)].bitcast(FP4X4),
                         lhsT_scale=w2s_perm[:, P * t : P * (t + 1)],
-                        rhs=u_codes[i][:].bitcast(FP8X4),
-                        rhs_scale=u_scl[i][:],
+                        rhs=u_codes[:, 256 * i : 256 * (i + 1)].bitcast(FP8X4),
+                        rhs_scale=u_scl[:, 256 * i : 256 * (i + 1)],
                         start=True,
                         stop=True,
                     )
@@ -245,7 +249,7 @@ def tile_gin_pc_w4_kernel(
                 )
 
         def interleave_h2(i):
-            nc.vector.tensor_copy(out=h2_grp[i][:], in_=h2_flat[i][:].rearrange("p t n -> p n t"))
+            nc.vector.tensor_copy(out=h2_grp[i][:], in_=h2_flat[i].rearrange("p t n -> p n t"))
 
         def make_ident_bf16():
             nc.vector.tensor_copy(out=ident_bf[:], in_=ident[:])
@@ -253,7 +257,7 @@ def tile_gin_pc_w4_kernel(
         def weave_h2(i, k):
             bank = psum.tile([P, 2, HID], BF16, name=f"bank{k}", tag=f"bank{k}")
             banks["weave", i] = bank
-            woven = h2_flat[i][:].rearrange("p t n -> p n t")
+            woven = h2_flat[i].rearrange("p t n -> p n t")
             for b in range(2):
                 nc.tensor.matmul(bank[:, b, :], lhsT=ident_bf[:], rhs=woven[:, b * P : (b + 1) * P, :], start=True, stop=True)
 
@@ -303,10 +307,6 @@ def tile_gin_pc_w4_kernel(
         def max_pair(i):
             nc.vector.tensor_reduce(out=nmax[:, 2 * i : 2 * i + 2], in_=lt_sb[i][:], axis=AX, op=MAX, negate=True)
 
-        def finish_rows_scalar(i, b):
-            n = 2 * i + b
-            nc.scalar.activation(out=res[i][:, b, :], in_=lt_sb[i][:, b, :], func=IDENT, bias=shift[:, n : n + 1])
-
         def bias_rows(i, b):
             nc.vector.tensor_tensor(out=lt_sb[i][:, b, :], in0=banks["rows", i, b][:], in1=bo_all[:], op=ADD)
 
@@ -349,12 +349,6 @@ def tile_gin_pc_w4_kernel(
                 scale=ssum[:, n : n + 1],
                 bias=LOG_STEP,
                 accum_out=tsum[:, n : n + 1],
-            )
-
-        def make_shift(i):
-            cols = slice(2 * i, 2 * i + 2)
-            nc.vector.scalar_tensor_tensor(
-                out=shift[:, cols], in0=tsum[:, cols], scalar=-LOG_CONST, in1=nmax[:, cols], op0=ADD, op1=ADD
             )
 
         def store(i, b0, b1):
@@ -440,30 +434,30 @@ def tile_gin_pc_w4_kernel(
         exp_rows(1, 1)
         quantize_hg(3)
         matmul_rows(3, 0, (0, 1), 5)
-        quantize_h2(3)
-        matmul_rows(3, 1, (0, 1), 0)
-        bias_pair(2)
-        matmul_rows(3, 0, (2,))
-        make_shift(0)
-        matmul_rows(3, 1, (2,))
-        finish_rows_scalar(0, 0)
-        max_pair(2)
         log_terms(1, 0)
         log_terms(1, 1)
-        bias_rows(3, 0)
-        finish_rows_scalar(0, 1)
-        bias_rows(3, 1)
-        store(0, 0, 2)
+        bias_pair(2)
+        matmul_rows(3, 1, (0, 1), 0)
+        offset_max(0, 4)
+        quantize_h2(3)
+        matmul_rows(3, 0, (2,))
+        max_pair(2)
+        matmul_rows(3, 1, (2,))
         exp_rows(2, 0)
         exp_rows(2, 1)
-        offset_max(2, 6)
+        finish_rows(0, 0)
+        finish_rows(0, 1)
+        store(0, 0, 2)
         log_terms(2, 0)
         log_terms(2, 1)
+        bias_rows(3, 0)
+        bias_rows(3, 1)
+        offset_max(4, 6)
         max_rows(3, 0)
         exp_rows(3, 0)
+        finish_rows(1, 0)
         max_rows(3, 1)
         exp_rows(3, 1)
-        finish_rows(1, 0)
         finish_rows(1, 1)
         store(1, 0, 2)
         log_terms(3, 0)

@@ -167,9 +167,16 @@ def tile_gin_pc_w4_kernel(
             for j in range(4):
                 nc.tensor.transpose(bank[:, j, :], scale_col[:, j : j + 1].to_broadcast([P, P]), ident[:])
 
-        def spread_scale():
-            nc.scalar.copy(
-                out=scale_all[:].rearrange("p (n j) -> p n j", j=4), in_=banks["scale"][:].rearrange("p j n -> p n j")
+        def spread_scale_half_vector(c):
+            nc.vector.tensor_copy(
+                out=scale_all[:, 256 * c : 256 * (c + 1)].rearrange("p (n j) -> p n j", j=4),
+                in_=banks["scale"][:, :, 64 * c : 64 * (c + 1)].rearrange("p j n -> p n j"),
+            )
+
+        def widen_half(c):
+            cols = slice(256 * c, 256 * (c + 1))
+            nc.vector.tensor_tensor(
+                out=u_val[0][:, cols], in0=pair_of(u_raw, U_LOADS, 0)[:, cols].bitcast(FP8), in1=scale_all[:, cols], op=MULT
             )
 
         def permute_w2_words():
@@ -356,7 +363,6 @@ def tile_gin_pc_w4_kernel(
 
         make_nodes()
         turn_scale(0)
-        spread_scale()
         turn("h", 0, 1)
         group("h", 0)
         make_ident_bf16()
@@ -365,7 +371,10 @@ def tile_gin_pc_w4_kernel(
         permute_w2_words()
         turn("h", 1, 3)
         group("h", 1)
-        widen(0, 0)
+        spread_scale_half_vector(0)
+        spread_scale_half_vector(1)
+        widen_half(0)
+        widen_half(1)
         widen(0, 1)
         turn("u", 0, 0)
         group("u", 0)
@@ -467,6 +476,5 @@ def tile_gin_pc_w4_kernel(
         finish_rows(2, 1)
         store(2, 0, 2)
         finish_rows(3, 0)
-        store(3, 0, 1)
         finish_rows(3, 1)
-        store(3, 1, 2)
+        store(3, 0, 2)

@@ -71,6 +71,7 @@ def tile_gin_pc_w4_kernel(
         wo = sb([P, 3, 2 * CLS], U8, "wo")
         wos = sb([P, 3, CLS], U8, "wos")
         ident = sb([P, P], F32, "ident")
+        warm = sb([P, HID], BF16, "warm")
         ident_bf = sb([P, P], BF16, "ident_bf")
         scale_all = sb([P, HID], F32, "scale_all")
         ones = sb([P, TERMS], F32, "ones")
@@ -124,6 +125,7 @@ def tile_gin_pc_w4_kernel(
             for r in range(4):
                 nc.sync.dma_start(out=wos[r:P:32, :, :].bitcast(I32), in_=wos_hbm[r].bitcast(I32))
 
+        nc.gpsimd.memset(warm[:].bitcast(I32), 0)
         make_identity(nc, ident[:])
         nc.vector.memset(w2s_in[:].bitcast(I32), 0)
         nc.vector.memset(wos[:].rearrange("p g n -> p (g n)").bitcast(I32), 0)
@@ -160,6 +162,17 @@ def tile_gin_pc_w4_kernel(
             )
             nc.scalar.activation(out=node_x[:], in_=node_t[:], func=EXP)
             nc.vector.tensor_scalar(out=node_neg[:], in0=node_x[:], scalar1=-1.0, scalar2=None, op0=MULT)
+
+        def warm_up(count, k):
+            bank = take_bank(k, [P, 256])
+            words = warm[:].bitcast(F32)
+            for step in range(count):
+                nc.tensor.matmul(bank[:], lhsT=words[:, :P], rhs=words, start=True, stop=True)
+
+        def warm_up_first(count, k):
+            bank = take_bank(k, [P, HID])
+            for step in range(count):
+                nc.tensor.matmul(bank[:], lhsT=warm[:, :P], rhs=warm[:], start=True, stop=True)
 
         def turn_scale(k):
             bank = take_bank(k, [P, 4, P])
@@ -362,17 +375,19 @@ def tile_gin_pc_w4_kernel(
             nc.sync.dma_start(out=o_hbm[:, 2 * i + b0 : 2 * i + b1, :], in_=res[i][:, b0:b1, :])
 
         make_nodes()
+        warm_up_first(4, 7)
         turn_scale(0)
+        make_ident_bf16()
         turn("h", 0, 1)
         group("h", 0)
-        make_ident_bf16()
+        permute_w2_words()
         turn("g", 0, 2)
         group("g", 0)
-        permute_w2_words()
+        spread_scale_half_vector(0)
+        warm_up(1, 7)
+        spread_scale_half_vector(1)
         turn("h", 1, 3)
         group("h", 1)
-        spread_scale_half_vector(0)
-        spread_scale_half_vector(1)
         widen_half(0)
         widen_half(1)
         widen(0, 1)
@@ -380,34 +395,35 @@ def tile_gin_pc_w4_kernel(
         group("u", 0)
         widen(1, 0)
         widen(1, 1)
+        warm_up(1, 7)
+        quantize_hg(0)
         turn("g", 1, 1)
         group("g", 1)
-        quantize_hg(0)
+        quantize_u(0)
         turn("u", 1, 2)
         group("u", 1)
-        quantize_u(0)
+        permute_w2_scales()
         turn("h", 2, 3)
         group("h", 2)
-        permute_w2_scales()
+        widen(2, 0)
+        widen(2, 1)
         matmul_h2_pair(0, (4, 5))
         bias_h2_planes(0, 0)
         bias_h2_planes(0, 1)
-        widen(2, 0)
-        widen(2, 1)
+        quantize_u(1)
         turn("u", 2, 0)
         group("u", 2)
-        quantize_u(1)
+        widen(3, 0)
+        widen(3, 1)
         matmul_h2_pair(1, (4, 5))
         bias_h2_planes(1, 0)
         bias_h2_planes(1, 1)
-        widen(3, 0)
-        widen(3, 1)
+        quantize_hg(1)
         turn("u", 3, 1)
         group("u", 3)
-        quantize_hg(1)
+        interleave_h2(0)
         turn("g", 2, 2)
         group("g", 2)
-        interleave_h2(0)
         quantize_u(2)
         matmul_h2_pair(2, (4, 5))
         bias_h2_planes(2, 0)

@@ -144,9 +144,9 @@ def tile_gin_pc_w4_kernel(
         nc.sync.dma_start(out=b2_col[:], in_=b2_1.rearrange("(p t) -> p t", t=4))
         load_g(2)
         nc.sync.dma_start(out=wo[:], in_=wo_words.rearrange("g p n -> p g n"))
+        load_wo_scales()
         load_h(3)
         load_g(3)
-        load_wo_scales()
         nc.sync.dma_start(out=bo_all[:], in_=b_out.partition_broadcast(P))
 
         banks = {}
@@ -395,14 +395,14 @@ def tile_gin_pc_w4_kernel(
         group("u", 0)
         widen(1, 0)
         widen(1, 1)
-        warm_up(1, 7)
-        quantize_hg(0)
         turn("g", 1, 1)
         group("g", 1)
-        quantize_u(0)
+        quantize_hg(0)
+        warm_up(1, 7)
+        permute_w2_scales()
         turn("u", 1, 2)
         group("u", 1)
-        permute_w2_scales()
+        quantize_u(0)
         turn("h", 2, 3)
         group("h", 2)
         widen(2, 0)
@@ -415,54 +415,57 @@ def tile_gin_pc_w4_kernel(
         group("u", 2)
         widen(3, 0)
         widen(3, 1)
-        matmul_h2_pair(1, (4, 5))
+        matmul_h2_pair(1, (6, 7))
         bias_h2_planes(1, 0)
         bias_h2_planes(1, 1)
         quantize_hg(1)
+        turn("g", 2, 2)
+        interleave_h2(0)
         turn("u", 3, 1)
         group("u", 3)
-        interleave_h2(0)
-        turn("g", 2, 2)
-        group("g", 2)
         quantize_u(2)
+        matmul_pair_rows(0, (0, 1), 0)
+        group("g", 2)
+        quantize_h2(0)
         matmul_h2_pair(2, (4, 5))
         bias_h2_planes(2, 0)
         bias_h2_planes(2, 1)
-        quantize_h2(0)
-        matmul_pair_rows(0, (0, 1, 2), 6)
         interleave_h2(1)
+        matmul_pair_rows(0, (2,))
         quantize_u(3)
-        matmul_h2_pair(3, (0, 1))
+        matmul_pair_rows(1, (0, 1), 6)
+        quantize_h2(1)
+        matmul_h2_pair(3, (1, 2))
         bias_h2_planes(3, 0)
         bias_h2_planes(3, 1)
-        quantize_h2(1)
-        matmul_pair_rows(1, (0, 1, 2), 7)
         quantize_hg(2)
-        turn("h", 3, 2)
-        group("h", 3)
+        matmul_pair_rows(1, (2,))
         bias_pair(0)
-        turn("g", 3, 3)
-        group("g", 3)
+        turn("h", 3, 3)
+        group("h", 3)
         interleave_h2(2)
-        weave_h2(3, 4)
-        copy_weave(3)
+        turn("g", 3, 7)
+        group("g", 3)
         max_pair(0)
+        matmul_pair_rows(2, (0, 1), 5)
         exp_rows(0, 0)
-        exp_rows(0, 1)
         bias_pair(1)
+        weave_h2(3, 4)
+        exp_rows(0, 1)
+        quantize_h2(2)
+        matmul_pair_rows(2, (2,))
+        copy_weave(3)
+        max_pair(1)
         log_terms(0, 0)
         log_terms(0, 1)
-        quantize_h2(2)
-        matmul_pair_rows(2, (0, 1, 2), 6)
-        max_pair(1)
+        quantize_hg(3)
+        matmul_rows(3, 0, (0, 1), 3)
         exp_rows(1, 0)
         exp_rows(1, 1)
-        quantize_hg(3)
-        matmul_rows(3, 0, (0, 1), 5)
-        log_terms(1, 0)
-        log_terms(1, 1)
         bias_pair(2)
         matmul_rows(3, 1, (0, 1), 0)
+        log_terms(1, 0)
+        log_terms(1, 1)
         offset_max(0, 4)
         quantize_h2(3)
         matmul_rows(3, 0, (2,))
@@ -477,10 +480,10 @@ def tile_gin_pc_w4_kernel(
         log_terms(2, 1)
         bias_rows(3, 0)
         bias_rows(3, 1)
-        offset_max(4, 6)
+        finish_rows(1, 0)
         max_rows(3, 0)
         exp_rows(3, 0)
-        finish_rows(1, 0)
+        offset_max(4, 6)
         max_rows(3, 1)
         exp_rows(3, 1)
         finish_rows(1, 1)
@@ -492,5 +495,6 @@ def tile_gin_pc_w4_kernel(
         finish_rows(2, 1)
         store(2, 0, 2)
         finish_rows(3, 0)
+        store(3, 0, 1)
         finish_rows(3, 1)
-        store(3, 0, 2)
+        store(3, 1, 2)

@@ -71,7 +71,7 @@ def tile_gin_pc_w4_kernel(
         wo = sb([P, 3, 2 * CLS], U8, "wo")
         wos = sb([P, 3, CLS], U8, "wos")
         ident = sb([P, P], F32, "ident")
-        warm = sb([P, HID], BF16, "warm")
+        warm = sb([P, 2 * P], BF16, "warm")
         ident_bf = sb([P, P], BF16, "ident_bf")
         scale_all = sb([P, HID], F32, "scale_all")
         ones = sb([P, TERMS], F32, "ones")
@@ -164,15 +164,17 @@ def tile_gin_pc_w4_kernel(
             nc.vector.tensor_scalar(out=node_neg[:], in0=node_x[:], scalar1=-1.0, scalar2=None, op0=MULT)
 
         def warm_up(count, k):
-            bank = take_bank(k, [P, 256])
+            bank = take_bank(k, [P, 2, P])
             words = warm[:].bitcast(F32)
+            moving = words.unsqueeze(1).to_broadcast([P, 2, P])
             for step in range(count):
-                nc.tensor.matmul(bank[:], lhsT=words[:, :P], rhs=words, start=True, stop=True)
+                nc.tensor.matmul(bank[:], lhsT=words, rhs=moving, start=True, stop=True)
 
         def warm_up_first(count, k):
-            bank = take_bank(k, [P, HID])
+            bank = take_bank(k, [P, 2, 2 * P])
+            moving = warm[:].unsqueeze(1).to_broadcast([P, 2, 2 * P])
             for step in range(count):
-                nc.tensor.matmul(bank[:], lhsT=warm[:, :P], rhs=warm[:], start=True, stop=True)
+                nc.tensor.matmul(bank[:], lhsT=warm[:, :P], rhs=moving, start=True, stop=True)
 
         def turn_scale(k):
             bank = take_bank(k, [P, 4, P])
@@ -180,8 +182,8 @@ def tile_gin_pc_w4_kernel(
             for j in range(4):
                 nc.tensor.transpose(bank[:, j, :], scale_col[:, j : j + 1].to_broadcast([P, P]), ident[:])
 
-        def spread_scale_half_vector(c):
-            nc.vector.tensor_copy(
+        def spread_scale_half(c):
+            nc.scalar.copy(
                 out=scale_all[:, 256 * c : 256 * (c + 1)].rearrange("p (n j) -> p n j", j=4),
                 in_=banks["scale"][:, :, 64 * c : 64 * (c + 1)].rearrange("p j n -> p n j"),
             )
@@ -327,6 +329,10 @@ def tile_gin_pc_w4_kernel(
         def max_pair(i):
             nc.vector.tensor_reduce(out=nmax[:, 2 * i : 2 * i + 2], in_=lt_sb[i][:], axis=AX, op=MAX, negate=True)
 
+        def offset_max_scalar(i):
+            cols = slice(2 * i, 2 * i + 2)
+            nc.scalar.activation(out=shift[:, cols], in_=nmax[:, cols], func=IDENT, bias=-LOG_CONST)
+
         def bias_rows(i, b):
             nc.vector.tensor_tensor(out=lt_sb[i][:, b, :], in0=banks["rows", i, b][:], in1=bo_all[:], op=ADD)
 
@@ -342,11 +348,6 @@ def tile_gin_pc_w4_kernel(
                 func=EXP,
                 bias=nmax[:, n : n + 1],
                 accum_out=ssum[:, n : n + 1],
-            )
-
-        def offset_max(n0, n1):
-            nc.vector.tensor_scalar(
-                out=shift[:, n0:n1], in0=nmax[:, n0:n1], scalar1=-LOG_CONST, scalar2=None, op0=ADD
             )
 
         def finish_rows(i, b):
@@ -377,19 +378,19 @@ def tile_gin_pc_w4_kernel(
         make_nodes()
         warm_up_first(4, 7)
         turn_scale(0)
+        spread_scale_half(0)
         make_ident_bf16()
         turn("h", 0, 1)
-        group("h", 0)
+        spread_scale_half(1)
         permute_w2_words()
         turn("g", 0, 2)
-        group("g", 0)
-        spread_scale_half_vector(0)
+        group("h", 0)
+        widen_half(0)
         warm_up(1, 7)
-        spread_scale_half_vector(1)
+        group("g", 0)
+        widen_half(1)
         turn("h", 1, 3)
         group("h", 1)
-        widen_half(0)
-        widen_half(1)
         widen(0, 1)
         turn("u", 0, 0)
         group("u", 0)
@@ -456,41 +457,42 @@ def tile_gin_pc_w4_kernel(
         matmul_pair_rows(2, (2,))
         copy_weave(3)
         max_pair(1)
-        log_terms(0, 0)
-        log_terms(0, 1)
+        offset_max_scalar(0)
         quantize_hg(3)
         matmul_rows(3, 0, (0, 1), 3)
-        exp_rows(1, 0)
-        exp_rows(1, 1)
+        log_terms(0, 0)
+        log_terms(0, 1)
         bias_pair(2)
         matmul_rows(3, 1, (0, 1), 0)
-        log_terms(1, 0)
-        log_terms(1, 1)
-        offset_max(0, 4)
+        exp_rows(1, 0)
+        exp_rows(1, 1)
         quantize_h2(3)
         matmul_rows(3, 0, (2,))
+        offset_max_scalar(1)
         max_pair(2)
         matmul_rows(3, 1, (2,))
-        exp_rows(2, 0)
-        exp_rows(2, 1)
+        log_terms(1, 0)
+        log_terms(1, 1)
         finish_rows(0, 0)
         finish_rows(0, 1)
         store(0, 0, 2)
+        exp_rows(2, 0)
+        exp_rows(2, 1)
+        bias_rows(3, 0)
+        offset_max_scalar(2)
+        bias_rows(3, 1)
         log_terms(2, 0)
         log_terms(2, 1)
-        bias_rows(3, 0)
-        bias_rows(3, 1)
-        finish_rows(1, 0)
         max_rows(3, 0)
         exp_rows(3, 0)
-        offset_max(4, 6)
         max_rows(3, 1)
         exp_rows(3, 1)
+        finish_rows(1, 0)
+        offset_max_scalar(3)
         finish_rows(1, 1)
         store(1, 0, 2)
         log_terms(3, 0)
         log_terms(3, 1)
-        offset_max(6, 8)
         finish_rows(2, 0)
         finish_rows(2, 1)
         store(2, 0, 2)

@@ -10,6 +10,7 @@ F32 = mybir.dt.float32
 BF16 = mybir.dt.bfloat16
 I32 = mybir.dt.int32
 U32 = mybir.dt.uint32
+U16 = mybir.dt.uint16
 U8 = mybir.dt.uint8
 FP8 = mybir.dt.float8_e4m3fn
 FP8X4 = mybir.dt.float8_e4m3fn_x4
@@ -33,10 +34,9 @@ T0 = 3.25 - (TERMS - 1) * STEP
 T_TAIL = T0 + STEP - math.log(math.exp(STEP) - 1.0)
 LOG_CONST = STEP * (math.exp(-math.exp(T_TAIL)) + sum(math.exp(-math.exp(T0 + j * STEP)) for j in range(1, TERMS)))
 
-U_LOADS = ((0, 1), (1, 1), (2, 2))
+U_LOADS = ((0, 1), (1, 1), (2, 1), (3, 1))
 H_LOADS = ((0, 1), (1, 1), (2, 1), (3, 1))
 G_LOADS = ((0, 1), (1, 1), (2, 1), (3, 1))
-H2_UNITS = ((0, 1), (1, 1), (2, 1), (3, 1))
 
 
 def tile_gin_pc_w4_kernel(
@@ -71,27 +71,21 @@ def tile_gin_pc_w4_kernel(
         wo = sb([P, 3, 2 * CLS], U8, "wo")
         wos = sb([P, 3, CLS], U8, "wos")
         ident = sb([P, P], F32, "ident")
-        warm = sb([P, 2 * P], BF16, "warm")
-        ident_bf = sb([P, P], BF16, "ident_bf")
-        scale_all = sb([P, HID], F32, "scale_all")
         ones = sb([P, TERMS], F32, "ones")
         count = sb([P, TERMS], F32, "count")
         node_t = sb([P, TERMS], F32, "node_t")
         node_x = sb([P, TERMS], F32, "node_x")
         node_neg = sb([P, TERMS], F32, "node_neg")
-        u_val = [sb([P, HID], BF16, f"u_val{n}") for n in range(NB)]
-        u_grp_all = sb([P, 4 * NODES], BF16, "u_grp")
-        u_grp = [u_grp_all[:, 1024 * i : 1024 * (i + 1)].rearrange("p (n t) -> p n t", t=4) for i in range(NP)]
+        u_wide = [sb([P, 2 * HID], BF16, f"u_wide{i}") for i in range(NP)]
+        u_grp = [sb([P, 256, 4], BF16, f"u_grp{i}") for i in range(NP)]
         hg_grp = [sb([P, 2, 256, 4], BF16, f"hg_grp{i}") for i in range(NP)]
-        h2_grp = [sb([P, 256, 4], BF16, f"h2_grp{i}") for i in range(NP)]
-        u_codes = sb([P, NODES], U32, "u_codes")
-        u_scl = sb([P, NODES], U8, "u_scl")
+        u_codes = [sb([P, 256], U32, f"u_codes{i}") for i in range(NP)]
+        u_scl = [sb([P, 256], U8, f"u_scl{i}") for i in range(NP)]
         hg_codes = [sb([P, 512], U32, f"hg_codes{i}") for i in range(NP)]
         hg_scl = [sb([P, 512], U8, f"hg_scl{i}") for i in range(NP)]
         h2_codes = [sb([P, 256], U32, f"h2_codes{i}") for i in range(NP)]
         h2_scl = [sb([P, 256], U8, f"h2_scl{i}") for i in range(NP)]
-        planes = {i: sb([P, 4, 256 * n], BF16, f"planes{i}") for i, n in H2_UNITS}
-        h2_flat = [planes[f][:, :, 256 * (i - f) : 256 * (i - f + 1)] for f, n in H2_UNITS for i in range(f, f + n)]
+        planes = [sb([P, 4, 256], BF16, f"planes{i}") for i in range(NP)]
         bo_all = sb([P, CLS], BF16, "bo_all")
         lt_sb = [sb([P, 2, 256], F32, f"lt_sb{i}") for i in range(NP)]
         terms = [sb([P, TERMS], F32, f"terms{n}") for n in range(NB)]
@@ -100,6 +94,7 @@ def tile_gin_pc_w4_kernel(
         tsum = sb([P, NB], F32, "tsum")
         shift = sb([P, NB], F32, "shift")
         res = [sb([P, 2, CLS], F32, f"res{i}") for i in range(NP)]
+        h2_grp = [u_grp[1][:], u_grp[0][:], hg_grp[1][:, 0], u_grp[2][:]]
 
         u_hbm = u1_bytes.rearrange("(p i b) k -> p i (b k)", i=NP, b=2)
         h_hbm = h.rearrange("(p i b) k -> p i (b k)", i=NP, b=2)
@@ -115,39 +110,30 @@ def tile_gin_pc_w4_kernel(
         def load_g(i):
             nc.sync.dma_start(out=g_sb[i][:], in_=g_hbm[:, i : i + dict(G_LOADS)[i], :].bitcast(F32))
 
-        def load_w2_scales():
+        def load_scale():
+            nc.sync.dma_start(out=scale_col[:], in_=u1_scale.rearrange("o (p j) -> p (o j)", j=4))
+
+        def load_w2():
+            nc.sync.dma_start(out=w2_in[:], in_=w2_words[0])
+
+        def load_b2():
+            nc.sync.dma_start(out=b2_col[:], in_=b2_1.rearrange("(p t) -> p t", t=4))
+
+        def load_wo():
+            nc.sync.dma_start(out=wo[:], in_=wo_words.rearrange("g p n -> p g n"))
+
+        def load_bo():
+            nc.sync.dma_start(out=bo_all[:], in_=b_out.partition_broadcast(P))
+
+        def load_w2_scales(queue):
             w2s_hbm = w2_scales[0].rearrange("(q r) n -> r q n", r=4)
             for r in range(4):
-                nc.sync.dma_start(out=w2s_in[r:P:32, :].bitcast(I32), in_=w2s_hbm[r].bitcast(I32))
+                queue.dma_start(out=w2s_in[r:P:32, :].bitcast(I32), in_=w2s_hbm[r].bitcast(I32))
 
-        def load_wo_scales():
+        def load_wo_scales(queue):
             wos_hbm = wo_scales.rearrange("g (q r) n -> r q g n", r=4)
             for r in range(4):
-                nc.sync.dma_start(out=wos[r:P:32, :, :].bitcast(I32), in_=wos_hbm[r].bitcast(I32))
-
-        nc.gpsimd.memset(warm[:].bitcast(I32), 0)
-        make_identity(nc, ident[:])
-        nc.vector.memset(w2s_in[:].bitcast(I32), 0)
-        nc.vector.memset(wos[:].rearrange("p g n -> p (g n)").bitcast(I32), 0)
-
-        nc.sync.dma_start(out=scale_col[:], in_=u1_scale.rearrange("o (p j) -> p (o j)", j=4))
-        nc.sync.dma_start(out=w2_in[:], in_=w2_words[0])
-        load_h(0)
-        load_g(0)
-        load_u(0)
-        load_h(1)
-        load_u(1)
-        load_g(1)
-        load_w2_scales()
-        load_u(2)
-        load_h(2)
-        nc.sync.dma_start(out=b2_col[:], in_=b2_1.rearrange("(p t) -> p t", t=4))
-        load_g(2)
-        nc.sync.dma_start(out=wo[:], in_=wo_words.rearrange("g p n -> p g n"))
-        load_wo_scales()
-        load_h(3)
-        load_g(3)
-        nc.sync.dma_start(out=bo_all[:], in_=b_out.partition_broadcast(P))
+                queue.dma_start(out=wos[r:P:32, :, :].bitcast(I32), in_=wos_hbm[r].bitcast(I32))
 
         banks = {}
 
@@ -161,44 +147,9 @@ def tile_gin_pc_w4_kernel(
                 out=node_t[:, 0:1], in0=ones[:, 0:1], scalar1=T_TAIL, scalar2=None, op0=MULT
             )
             nc.scalar.activation(out=node_x[:], in_=node_t[:], func=EXP)
+
+        def negate_nodes():
             nc.vector.tensor_scalar(out=node_neg[:], in0=node_x[:], scalar1=-1.0, scalar2=None, op0=MULT)
-
-        def warm_up(count, k):
-            bank = take_bank(k, [P, 2, P])
-            words = warm[:].bitcast(F32)
-            moving = words.unsqueeze(1).to_broadcast([P, 2, P])
-            for step in range(count):
-                nc.tensor.matmul(bank[:], lhsT=words, rhs=moving, start=True, stop=True)
-
-        def warm_up_first(count, k):
-            bank = take_bank(k, [P, 2, 2 * P])
-            moving = warm[:].unsqueeze(1).to_broadcast([P, 2, 2 * P])
-            for step in range(count):
-                nc.tensor.matmul(bank[:], lhsT=warm[:, :P], rhs=moving, start=True, stop=True)
-
-        def turn_scale(k):
-            bank = take_bank(k, [P, 4, P])
-            banks["scale"] = bank
-            for j in range(4):
-                nc.tensor.transpose(bank[:, j, :], scale_col[:, j : j + 1].to_broadcast([P, P]), ident[:])
-
-        def spread_scale_half(c):
-            nc.scalar.copy(
-                out=scale_all[:, 256 * c : 256 * (c + 1)].rearrange("p (n j) -> p n j", j=4),
-                in_=banks["scale"][:, :, 64 * c : 64 * (c + 1)].rearrange("p j n -> p n j"),
-            )
-
-        def widen_half(c):
-            cols = slice(256 * c, 256 * (c + 1))
-            nc.vector.tensor_tensor(
-                out=u_val[0][:, cols], in0=pair_of(u_raw, U_LOADS, 0)[:, cols].bitcast(FP8), in1=scale_all[:, cols], op=MULT
-            )
-
-        def permute_w2_words():
-            nc.vector.tensor_copy(
-                out=w2_perm[:].rearrange("p (t m b) -> p t m b", t=4, b=2),
-                in_=w2_in[:].rearrange("p (m t b) -> p t m b", t=4, b=2),
-            )
 
         def permute_w2_scales():
             nc.vector.tensor_copy(
@@ -207,47 +158,52 @@ def tile_gin_pc_w4_kernel(
             )
 
 
-        def widen(i, b):
+        def cast_scalar(i, b0, b1):
+            cols = slice(b0 * HID, b1 * HID)
+            nc.scalar.copy(out=u_wide[i][:, cols], in_=pair_of(u_raw, U_LOADS, i)[:, cols].bitcast(FP8))
+
+        def cast_vector(i, b0, b1):
+            cols = slice(b0 * HID, b1 * HID)
+            nc.vector.tensor_copy(out=u_wide[i][:, cols], in_=pair_of(u_raw, U_LOADS, i)[:, cols].bitcast(FP8))
+
+        def turn(x, i, k):
+            bank = take_bank(k, [P, 2, 2 * P])
+            banks[x, i] = bank
+            if x == "u":
+                rows = u_wide[i][:].bitcast(F32)
+            else:
+                rows = pair_of(h_sb, H_LOADS, i) if x == "h" else pair_of(g_sb, G_LOADS, i)
+            for b in range(2):
+                for e in range(2):
+                    nc.tensor.transpose(bank[:, e, b * P : (b + 1) * P], rows[:, b * 256 + e : (b + 1) * 256 : 2], ident[:])
+
+        def scale_u(i):
             nc.vector.tensor_tensor(
-                out=u_val[2 * i + b][:],
-                in0=pair_of(u_raw, U_LOADS, i)[:, b * HID : (b + 1) * HID].bitcast(FP8),
-                in1=scale_all[:],
+                out=u_grp[i][:].rearrange("p n (e j) -> p n e j", e=2),
+                in0=banks["u", i][:].bitcast(BF16).rearrange("p e (n j) -> p n e j", j=2),
+                in1=scale_col[:].rearrange("p (e j) -> p e j", e=2).unsqueeze(1).to_broadcast([P, 256, 2, 2]),
                 op=MULT,
             )
 
-        def turn(x, i, k):
-            bank = take_bank(k, [P, 2, 2, P])
-            banks[x, i] = bank
-            for b in range(2):
-                if x == "u":
-                    words = u_val[2 * i + b][:].bitcast(F32)
-                else:
-                    rows = pair_of(h_sb, H_LOADS, i) if x == "h" else pair_of(g_sb, G_LOADS, i)
-                    words = rows[:, b * 256 : (b + 1) * 256]
-                for e in range(2):
-                    nc.tensor.transpose(bank[:, b, e, :], words[:, e:256:2], ident[:])
+        def grouped_words(x, i):
+            return hg_grp[i][:, 0 if x == "h" else 1].bitcast(F32)
 
         def group(x, i):
-            dst = u_grp[i] if x == "u" else hg_grp[i][:, 0 if x == "h" else 1]
-            nc.scalar.copy(
-                out=dst.rearrange("p (b n) t -> p b n t", b=2).bitcast(F32),
-                in_=banks[x, i][:].rearrange("p b e n -> p b n e"),
-            )
+            nc.scalar.copy(out=grouped_words(x, i), in_=banks[x, i][:].rearrange("p e n -> p n e"))
 
         def quantize(codes, scl, grp):
             nc.vector.quantize_mx(out=codes[:].bitcast(FP8X4), scales=scl[:], in_=grp)
 
         def quantize_u(i):
-            nodes = slice(256 * i, 256 * (i + 1))
-            quantize(u_codes[:, nodes], u_scl[:, nodes], u_grp_all[:, 1024 * i : 1024 * (i + 1)])
+            quantize(u_codes[i], u_scl[i], u_grp[i][:].rearrange("p n t -> p (n t)"))
 
         def quantize_hg(i):
             quantize(hg_codes[i], hg_scl[i], hg_grp[i][:].rearrange("p s n t -> p (s n t)"))
 
         def quantize_h2(i):
-            quantize(h2_codes[i], h2_scl[i], h2_grp[i][:].rearrange("p n t -> p (n t)"))
+            quantize(h2_codes[i], h2_scl[i], h2_grp[i].rearrange("p n t -> p (n t)"))
 
-        def matmul_h2_pair(i, k):
+        def matmul_h2(i, k):
             for u in range(2):
                 bank = take_bank(k[u], [P, 2, 256])
                 banks["h2", i, u] = bank
@@ -257,54 +213,28 @@ def tile_gin_pc_w4_kernel(
                         out=bank[:, v, :],
                         lhsT=w2_perm[:, 2 * P * t : 2 * P * (t + 1)].bitcast(FP4X4),
                         lhsT_scale=w2s_perm[:, P * t : P * (t + 1)],
-                        rhs=u_codes[:, 256 * i : 256 * (i + 1)].bitcast(FP8X4),
-                        rhs_scale=u_scl[:, 256 * i : 256 * (i + 1)],
+                        rhs=u_codes[i][:].bitcast(FP8X4),
+                        rhs_scale=u_scl[i][:],
                         start=True,
                         stop=True,
                     )
 
-        def bias_h2_planes(i, u):
+        def bias_h2(i, u):
             for v in range(2):
                 t = 2 * u + v
                 nc.scalar.activation(
-                    out=h2_flat[i][:, t, :], in_=banks["h2", i, u][:, v, :], func=IDENT, bias=b2_col[:, t : t + 1]
+                    out=planes[i][:, t, :], in_=banks["h2", i, u][:, v, :], func=IDENT, bias=b2_col[:, t : t + 1]
                 )
 
-        def interleave_h2(i):
-            nc.vector.tensor_copy(out=h2_grp[i][:], in_=h2_flat[i].rearrange("p t n -> p n t"))
+        def interleave_vector(i):
+            nc.vector.tensor_copy(out=h2_grp[i], in_=planes[i][:].rearrange("p t n -> p n t"))
 
-        def make_ident_bf16():
-            nc.vector.tensor_copy(out=ident_bf[:], in_=ident[:])
-
-        def weave_h2(i, k):
-            bank = psum.tile([P, 2, HID], BF16, name=f"bank{k}", tag=f"bank{k}")
-            banks["weave", i] = bank
-            woven = h2_flat[i].rearrange("p t n -> p n t")
-            for b in range(2):
-                nc.tensor.matmul(bank[:, b, :], lhsT=ident_bf[:], rhs=woven[:, b * P : (b + 1) * P, :], start=True, stop=True)
-
-        def copy_weave(i):
-            nc.scalar.copy(
-                out=h2_grp[i][:].rearrange("p n t -> p (n t)"), in_=banks["weave", i][:].rearrange("p b k -> p (b k)")
+        def interleave_gpsimd(i):
+            nc.gpsimd.tensor_scalar(
+                out=h2_grp[i], in0=planes[i][:].rearrange("p t n -> p n t"), scalar1=1.0, scalar2=0.0, op0=MULT, op1=ADD
             )
 
-        def matmul_rows(i, b, groups, k=None):
-            if groups[0] == 0:
-                banks["rows", i, b] = take_bank(k, [P, CLS])
-            for g in groups:
-                codes, scl = (hg_codes[i], hg_scl[i]) if g < 2 else (h2_codes[i], h2_scl[i])
-                nodes = slice(256 * (g % 2) * (g < 2) + b * P, 256 * (g % 2) * (g < 2) + (b + 1) * P)
-                nc.tensor.matmul_mx(
-                    out=banks["rows", i, b][:],
-                    lhsT=codes[:, nodes].bitcast(FP8X4),
-                    lhsT_scale=scl[:, nodes],
-                    rhs=wo[:, g, :].bitcast(FP4X4),
-                    rhs_scale=wos[:, g, :],
-                    start=(g == 0),
-                    stop=(g == 2),
-                )
-
-        def matmul_pair_rows(i, groups, k=None):
+        def matmul_pair(i, groups, k=None):
             if groups[0] == 0:
                 banks["rows", i] = take_bank(k, [P, 2, CLS])
             for g in groups:
@@ -321,6 +251,22 @@ def tile_gin_pc_w4_kernel(
                         stop=(g == 2 and b == 1),
                     )
 
+        def matmul_block(i, b, groups, k=None):
+            if groups[0] == 0:
+                banks["rows", i, b] = take_bank(k, [P, CLS])
+            for g in groups:
+                codes, scl = (hg_codes[i], hg_scl[i]) if g < 2 else (h2_codes[i], h2_scl[i])
+                nodes = slice(256 * (g % 2) + b * P, 256 * (g % 2) + (b + 1) * P)
+                nc.tensor.matmul_mx(
+                    out=banks["rows", i, b][:],
+                    lhsT=codes[:, nodes].bitcast(FP8X4),
+                    lhsT_scale=scl[:, nodes],
+                    rhs=wo[:, g, :].bitcast(FP4X4),
+                    rhs_scale=wos[:, g, :],
+                    start=(g == 0),
+                    stop=(g == 2),
+                )
+
         def bias_pair(i):
             nc.vector.tensor_tensor(
                 out=lt_sb[i][:], in0=banks["rows", i][:], in1=bo_all[:].unsqueeze(1).to_broadcast([P, 2, CLS]), op=ADD
@@ -329,18 +275,18 @@ def tile_gin_pc_w4_kernel(
         def max_pair(i):
             nc.vector.tensor_reduce(out=nmax[:, 2 * i : 2 * i + 2], in_=lt_sb[i][:], axis=AX, op=MAX, negate=True)
 
-        def offset_max_scalar(i):
+        def offset_max(i):
             cols = slice(2 * i, 2 * i + 2)
             nc.scalar.activation(out=shift[:, cols], in_=nmax[:, cols], func=IDENT, bias=-LOG_CONST)
 
-        def bias_rows(i, b):
+        def bias_block(i, b):
             nc.vector.tensor_tensor(out=lt_sb[i][:, b, :], in0=banks["rows", i, b][:], in1=bo_all[:], op=ADD)
 
-        def max_rows(i, b):
+        def max_block(i, b):
             n = 2 * i + b
             nc.vector.tensor_reduce(out=nmax[:, n : n + 1], in_=lt_sb[i][:, b, :], axis=AX, op=MAX, negate=True)
 
-        def exp_rows(i, b):
+        def exp_block(i, b):
             n = 2 * i + b
             nc.scalar.activation(
                 out=res[i][:, b, :],
@@ -350,18 +296,7 @@ def tile_gin_pc_w4_kernel(
                 accum_out=ssum[:, n : n + 1],
             )
 
-        def finish_rows(i, b):
-            n = 2 * i + b
-            nc.vector.tensor_scalar(
-                out=res[i][:, b, :],
-                in0=lt_sb[i][:, b, :],
-                scalar1=shift[:, n : n + 1],
-                scalar2=tsum[:, n : n + 1],
-                op0=ADD,
-                op1=ADD,
-            )
-
-        def log_terms(i, b):
+        def log_block(i, b):
             n = 2 * i + b
             nc.scalar.activation(
                 out=terms[n][:],
@@ -372,131 +307,226 @@ def tile_gin_pc_w4_kernel(
                 accum_out=tsum[:, n : n + 1],
             )
 
+        def finish_block(i, b):
+            n = 2 * i + b
+            nc.vector.tensor_scalar(
+                out=res[i][:, b, :],
+                in0=lt_sb[i][:, b, :],
+                scalar1=shift[:, n : n + 1],
+                scalar2=tsum[:, n : n + 1],
+                op0=ADD,
+                op1=ADD,
+            )
+
         def store(i, b0, b1):
             nc.sync.dma_start(out=o_hbm[:, 2 * i + b0 : 2 * i + b1, :], in_=res[i][:, b0:b1, :])
 
+        warm = sb([P, 2 * P], BF16, "warm")
+
+        def warm_up_first(count, k):
+            bank = take_bank(k, [P, 2, 2 * P])
+            moving = warm[:].unsqueeze(1).to_broadcast([P, 2, 2 * P])
+            for step in range(count):
+                nc.tensor.matmul(bank[:], lhsT=warm[:, :P], rhs=moving, start=True, stop=True)
+
+        def warm_up(k):
+            bank = take_bank(k, [P, 2, P])
+            words = warm[:].bitcast(F32)
+            nc.tensor.matmul(bank[:], lhsT=words, rhs=words.unsqueeze(1).to_broadcast([P, 2, P]), start=True, stop=True)
+
+        def warm_up_short(k):
+            bank = take_bank(k, [P, P])
+            words = warm[:].bitcast(F32)
+            nc.tensor.matmul(bank[:], lhsT=words, rhs=words, start=True, stop=True)
+
+        def matmul_h2_half(i, u, k):
+            bank = take_bank(k, [P, 2, 256])
+            banks["h2", i, u] = bank
+            for v in range(2):
+                t = 2 * u + v
+                nc.tensor.matmul_mx(
+                    out=bank[:, v, :],
+                    lhsT=w2_perm[:, 2 * P * t : 2 * P * (t + 1)].bitcast(FP4X4),
+                    lhsT_scale=w2s_perm[:, P * t : P * (t + 1)],
+                    rhs=u_codes[i][:].bitcast(FP8X4),
+                    rhs_scale=u_scl[i][:],
+                    start=True,
+                    stop=True,
+                )
+
+        def cast_sorted(i, b):
+            nc.vector.tensor_scalar(
+                out=u_wide[i][:, b * HID : (b + 1) * HID].rearrange("p (e m j) -> p m e j", e=2, j=2),
+                in0=pair_of(u_raw, U_LOADS, i)[:, b * HID : (b + 1) * HID].bitcast(FP8),
+                scalar1=ones[:, 0:1],
+                scalar2=None,
+                op0=MULT,
+            )
+
+        def turn_sorted(i, k):
+            bank = take_bank(k, [P, 2, 2 * P])
+            banks["u", i] = bank
+            words = u_wide[i][:].bitcast(F32)
+            for b in range(2):
+                for e in range(2):
+                    first = (2 * b + e) * P
+                    nc.tensor.transpose(bank[:, e, b * P : (b + 1) * P], words[:, first : first + P], ident[:])
+
+        def permute_w2_words_scalar():
+            nc.scalar.copy(
+                out=w2_perm[:].bitcast(U16).rearrange("p (t m) -> p t m", t=4),
+                in_=w2_in[:].bitcast(U16).rearrange("p (m t) -> p t m", t=4),
+            )
+
+        def sum_shift(i):
+            cols = slice(2 * i, 2 * i + 2)
+            nc.vector.scalar_tensor_tensor(
+                out=shift[:, cols], in0=nmax[:, cols], scalar=-LOG_CONST, in1=tsum[:, cols], op0=ADD, op1=ADD
+            )
+
+        def finish_scalar(i, b):
+            n = 2 * i + b
+            nc.scalar.activation(out=res[i][:, b, :], in_=lt_sb[i][:, b, :], func=IDENT, bias=shift[:, n : n + 1])
+
+        ident_bf = sb([P, P], BF16, "ident_bf")
+
+        nc.gpsimd.memset(warm[:].bitcast(I32), 0)
+        make_identity(nc, ident[:])
+        nc.vector.memset(w2s_in[:].bitcast(I32), 0)
+        nc.vector.memset(wos[:].rearrange("p g n -> p (g n)").bitcast(I32), 0)
         make_nodes()
+        load_u(0)
+        load_scale()
+        load_u(1)
+        load_h(0)
+        load_u(2)
+        load_w2()
+        load_w2_scales(nc.sync)
+        load_g(0)
+        load_u(3)
+        load_b2()
+        load_h(1)
+        load_g(1)
+        load_wo()
+        load_wo_scales(nc.sync)
+        load_h(2)
+        load_g(2)
+        load_bo()
+        load_h(3)
+        load_g(3)
         warm_up_first(4, 7)
-        turn_scale(0)
-        spread_scale_half(0)
-        make_ident_bf16()
-        turn("h", 0, 1)
-        spread_scale_half(1)
-        permute_w2_words()
-        turn("g", 0, 2)
+        cast_scalar(2, 0, 2)
+        permute_w2_words_scalar()
+        cast_sorted(0, 0)
+        cast_sorted(0, 1)
+        turn_sorted(0, 0)
+        warm_up_short(7)
+        cast_sorted(1, 0)
+        cast_sorted(1, 1)
+        turn_sorted(1, 1)
+        warm_up_short(7)
+        turn("h", 0, 3)
+        turn("u", 2, 6)
+        warm_up_short(7)
         group("h", 0)
-        widen_half(0)
-        warm_up(1, 7)
-        group("g", 0)
-        widen_half(1)
-        turn("h", 1, 3)
-        group("h", 1)
-        widen(0, 1)
-        turn("u", 0, 0)
-        group("u", 0)
-        widen(1, 0)
-        widen(1, 1)
-        turn("g", 1, 1)
-        group("g", 1)
-        quantize_hg(0)
-        warm_up(1, 7)
+        cast_scalar(3, 0, 2)
+        scale_u(0)
+        negate_nodes()
         permute_w2_scales()
-        turn("u", 1, 2)
-        group("u", 1)
         quantize_u(0)
-        turn("h", 2, 3)
-        group("h", 2)
-        widen(2, 0)
-        widen(2, 1)
-        matmul_h2_pair(0, (4, 5))
-        bias_h2_planes(0, 0)
-        bias_h2_planes(0, 1)
+        matmul_h2(0, (4, 5))
+        turn("g", 0, 2)
+        turn("u", 3, 0)
+        bias_h2(0, 0)
+        bias_h2(0, 1)
+        group("g", 0)
+        scale_u(1)
         quantize_u(1)
-        turn("u", 2, 0)
-        group("u", 2)
-        widen(3, 0)
-        widen(3, 1)
-        matmul_h2_pair(1, (6, 7))
-        bias_h2_planes(1, 0)
-        bias_h2_planes(1, 1)
-        quantize_hg(1)
-        turn("g", 2, 2)
-        interleave_h2(0)
-        turn("u", 3, 1)
-        group("u", 3)
+        matmul_h2(1, (3, 7))
+        turn("h", 1, 1)
+        turn("g", 1, 4)
+        turn("h", 2, 5)
+        bias_h2(1, 0)
+        bias_h2(1, 1)
+        group("h", 1)
+        group("g", 1)
+        group("h", 2)
+        interleave_gpsimd(0)
+        scale_u(2)
+        scale_u(3)
         quantize_u(2)
-        matmul_pair_rows(0, (0, 1), 0)
-        group("g", 2)
+        matmul_h2(2, (2, 6))
+        bias_h2(2, 0)
+        bias_h2(2, 1)
+        quantize_hg(0)
         quantize_h2(0)
-        matmul_h2_pair(2, (4, 5))
-        bias_h2_planes(2, 0)
-        bias_h2_planes(2, 1)
-        interleave_h2(1)
-        matmul_pair_rows(0, (2,))
+        matmul_pair(0, (0, 1, 2), 0)
+        turn("g", 2, 3)
+        group("g", 2)
         quantize_u(3)
-        matmul_pair_rows(1, (0, 1), 6)
+        matmul_h2(3, (7, 1))
+        bias_h2(3, 0)
+        bias_h2(3, 1)
+        interleave_vector(1)
+        quantize_hg(1)
+        interleave_gpsimd(2)
         quantize_h2(1)
-        matmul_h2_pair(3, (1, 2))
-        bias_h2_planes(3, 0)
-        bias_h2_planes(3, 1)
-        quantize_hg(2)
-        matmul_pair_rows(1, (2,))
-        bias_pair(0)
-        turn("h", 3, 3)
+        matmul_pair(1, (0, 1, 2), 4)
+        turn("h", 3, 5)
+        turn("g", 3, 2)
         group("h", 3)
-        interleave_h2(2)
-        turn("g", 3, 7)
         group("g", 3)
+        bias_pair(0)
         max_pair(0)
-        matmul_pair_rows(2, (0, 1), 5)
-        exp_rows(0, 0)
+        exp_block(0, 0)
+        exp_block(0, 1)
+        log_block(0, 0)
+        log_block(0, 1)
         bias_pair(1)
-        weave_h2(3, 4)
-        exp_rows(0, 1)
+        quantize_hg(2)
+        matmul_pair(2, (0, 1), 6)
         quantize_h2(2)
-        matmul_pair_rows(2, (2,))
-        copy_weave(3)
+        matmul_pair(2, (2,))
         max_pair(1)
-        offset_max_scalar(0)
+        exp_block(1, 0)
+        exp_block(1, 1)
+        log_block(1, 0)
+        log_block(1, 1)
+        interleave_vector(3)
         quantize_hg(3)
-        matmul_rows(3, 0, (0, 1), 3)
-        log_terms(0, 0)
-        log_terms(0, 1)
-        bias_pair(2)
-        matmul_rows(3, 1, (0, 1), 0)
-        exp_rows(1, 0)
-        exp_rows(1, 1)
+        matmul_block(3, 0, (0, 1), 0)
+        matmul_block(3, 1, (0, 1), 3)
         quantize_h2(3)
-        matmul_rows(3, 0, (2,))
-        offset_max_scalar(1)
-        max_pair(2)
-        matmul_rows(3, 1, (2,))
-        log_terms(1, 0)
-        log_terms(1, 1)
-        finish_rows(0, 0)
-        finish_rows(0, 1)
+        matmul_block(3, 0, (2,))
+        matmul_block(3, 1, (2,))
+        sum_shift(0)
+        finish_scalar(0, 0)
+        finish_scalar(0, 1)
+        bias_pair(2)
         store(0, 0, 2)
-        exp_rows(2, 0)
-        exp_rows(2, 1)
-        bias_rows(3, 0)
-        offset_max_scalar(2)
-        bias_rows(3, 1)
-        log_terms(2, 0)
-        log_terms(2, 1)
-        max_rows(3, 0)
-        exp_rows(3, 0)
-        max_rows(3, 1)
-        exp_rows(3, 1)
-        finish_rows(1, 0)
-        offset_max_scalar(3)
-        finish_rows(1, 1)
+        sum_shift(1)
+        finish_scalar(1, 0)
+        finish_scalar(1, 1)
+        max_pair(2)
         store(1, 0, 2)
-        log_terms(3, 0)
-        log_terms(3, 1)
-        finish_rows(2, 0)
-        finish_rows(2, 1)
+        exp_block(2, 0)
+        exp_block(2, 1)
+        offset_max(2)
+        log_block(2, 0)
+        log_block(2, 1)
+        bias_block(3, 0)
+        bias_block(3, 1)
+        max_block(3, 0)
+        exp_block(3, 0)
+        max_block(3, 1)
+        exp_block(3, 1)
+        offset_max(3)
+        log_block(3, 0)
+        log_block(3, 1)
+        finish_block(2, 0)
+        finish_block(2, 1)
         store(2, 0, 2)
-        finish_rows(3, 0)
+        finish_block(3, 0)
         store(3, 0, 1)
-        finish_rows(3, 1)
+        finish_block(3, 1)
         store(3, 1, 2)

@@ -2,7 +2,6 @@ import math
 from contextlib import ExitStack
 
 import concourse.mybir as mybir
-from concourse.masks import make_identity
 
 FLOPS = 2 * 1024 * 512 * 512 + 2 * 1024 * 1536 * 256
 
@@ -70,10 +69,10 @@ def tile_gin_pc_w4_kernel(
         w2s_perm = sb([P, HID], U8, "w2s_perm")
         wo = sb([P, 3, 2 * CLS], U8, "wo")
         wos = sb([P, 3, CLS], U8, "wos")
+        zeros = sb([P, P], F32, "zeros")
         ident = sb([P, P], F32, "ident")
         ones = sb([P, TERMS], F32, "ones")
         count = sb([P, TERMS], F32, "count")
-        node_t = sb([P, TERMS], F32, "node_t")
         node_x = sb([P, TERMS], F32, "node_x")
         node_neg = sb([P, TERMS], F32, "node_neg")
         u_wide = [sb([P, 2 * HID], BF16, f"u_wide{i}") for i in range(NP)]
@@ -138,18 +137,12 @@ def tile_gin_pc_w4_kernel(
         banks = {}
 
         def make_nodes():
-            nc.vector.memset(ones[:], 1.0)
+            nc.scalar.activation(out=node_x[:, 0:1], in_=ones[:, 0:1], func=EXP, scale=T_TAIL)
             nc.vector.tensor_tensor_scan(out=count[:], data0=ones[:], data1=ones[:], initial=-1.0, op0=MULT, op1=ADD)
-            nc.vector.tensor_scalar(
-                out=node_t[:, 1:], in0=count[:, 1:], scalar1=STEP, scalar2=T0, op0=MULT, op1=ADD
-            )
-            nc.vector.tensor_scalar(
-                out=node_t[:, 0:1], in0=ones[:, 0:1], scalar1=T_TAIL, scalar2=None, op0=MULT
-            )
-            nc.scalar.activation(out=node_x[:], in_=node_t[:], func=EXP)
+            nc.scalar.activation(out=node_x[:, 1:], in_=count[:, 1:], func=EXP, scale=STEP, bias=T0)
 
         def negate_nodes():
-            nc.vector.tensor_scalar(out=node_neg[:], in0=node_x[:], scalar1=-1.0, scalar2=None, op0=MULT)
+            nc.scalar.activation(out=node_neg[:], in_=node_x[:], func=IDENT, scale=-1.0)
 
         def permute_w2_scales():
             nc.vector.tensor_copy(
@@ -321,22 +314,22 @@ def tile_gin_pc_w4_kernel(
         def store(i, b0, b1):
             nc.sync.dma_start(out=o_hbm[:, 2 * i + b0 : 2 * i + b1, :], in_=res[i][:, b0:b1, :])
 
-        warm = sb([P, 2 * P], BF16, "warm")
+        warm = zeros[:].bitcast(BF16)
 
         def warm_up_first(count, k):
             bank = take_bank(k, [P, 2, 2 * P])
-            moving = warm[:].unsqueeze(1).to_broadcast([P, 2, 2 * P])
+            moving = warm.unsqueeze(1).to_broadcast([P, 2, 2 * P])
             for step in range(count):
                 nc.tensor.matmul(bank[:], lhsT=warm[:, :P], rhs=moving, start=True, stop=True)
 
         def warm_up(k):
             bank = take_bank(k, [P, 2, P])
-            words = warm[:].bitcast(F32)
+            words = zeros[:]
             nc.tensor.matmul(bank[:], lhsT=words, rhs=words.unsqueeze(1).to_broadcast([P, 2, P]), start=True, stop=True)
 
         def warm_up_short(k):
             bank = take_bank(k, [P, P])
-            words = warm[:].bitcast(F32)
+            words = zeros[:]
             nc.tensor.matmul(bank[:], lhsT=words, rhs=words, start=True, stop=True)
 
         def matmul_h2_half(i, u, k):
@@ -390,9 +383,25 @@ def tile_gin_pc_w4_kernel(
 
         ident_bf = sb([P, P], BF16, "ident_bf")
 
-        nc.gpsimd.memset(warm[:].bitcast(I32), 0)
-        make_identity(nc, ident[:])
+        def turn_block(i, b, step, k):
+            bank = take_bank(k, [P, 2, P])
+            banks["u", i, b] = bank
+            words = u_wide[i][:, b * HID : (b + 1) * HID].bitcast(F32)
+            for e in range(2):
+                nc.tensor.transpose(bank[:, e, :], words[:, e:256:2] if step == 2 else words[:, e * P : (e + 1) * P], ident[:])
+
+        def scale_block(i, b):
+            nc.vector.tensor_tensor(
+                out=u_grp[i][:, b * P : (b + 1) * P, :].rearrange("p n (e j) -> p n e j", e=2),
+                in0=banks["u", i, b][:].bitcast(BF16).rearrange("p e (n j) -> p n e j", j=2),
+                in1=scale_col[:].rearrange("p (e j) -> p e j", e=2).unsqueeze(1).to_broadcast([P, P, 2, 2]),
+                op=MULT,
+            )
+
+        nc.gpsimd.memset(zeros[:], 0.0)
+        nc.gpsimd.affine_select(out=ident[:], in_=zeros[:], pattern=[[-1, P]], compare_op=mybir.AluOpType.not_equal, fill=1.0, base=0, channel_multiplier=1)
         nc.vector.memset(w2s_in[:].bitcast(I32), 0)
+        nc.vector.memset(ones[:], 1.0)
         nc.vector.memset(wos[:].rearrange("p g n -> p (g n)").bitcast(I32), 0)
         make_nodes()
         load_u(0)
@@ -415,23 +424,24 @@ def tile_gin_pc_w4_kernel(
         load_h(3)
         load_g(3)
         warm_up_first(4, 7)
+        cast_scalar(0, 1, 2)
+        negate_nodes()
         cast_scalar(2, 0, 2)
         permute_w2_words_scalar()
         cast_sorted(0, 0)
-        cast_sorted(0, 1)
-        turn_sorted(0, 0)
-        warm_up_short(7)
+        turn_block(0, 0, 1, 0)
+        turn_block(0, 1, 2, 2)
+        turn("h", 0, 3)
+        group("h", 0)
+        cast_scalar(3, 0, 2)
         cast_sorted(1, 0)
         cast_sorted(1, 1)
         turn_sorted(1, 1)
         warm_up_short(7)
-        turn("h", 0, 3)
         turn("u", 2, 6)
         warm_up_short(7)
-        group("h", 0)
-        cast_scalar(3, 0, 2)
-        scale_u(0)
-        negate_nodes()
+        scale_block(0, 0)
+        scale_block(0, 1)
         permute_w2_scales()
         quantize_u(0)
         matmul_h2(0, (4, 5))
@@ -450,7 +460,6 @@ def tile_gin_pc_w4_kernel(
         bias_h2(1, 1)
         group("h", 1)
         group("g", 1)
-        group("h", 2)
         interleave_gpsimd(0)
         scale_u(2)
         scale_u(3)
@@ -458,6 +467,7 @@ def tile_gin_pc_w4_kernel(
         matmul_h2(2, (2, 6))
         bias_h2(2, 0)
         bias_h2(2, 1)
+        group("h", 2)
         quantize_hg(0)
         quantize_h2(0)
         matmul_pair(0, (0, 1, 2), 0)
@@ -487,23 +497,24 @@ def tile_gin_pc_w4_kernel(
         matmul_pair(2, (0, 1), 6)
         quantize_h2(2)
         matmul_pair(2, (2,))
+        warm_up_short(7)
         max_pair(1)
         exp_block(1, 0)
         exp_block(1, 1)
         log_block(1, 0)
         log_block(1, 1)
         interleave_vector(3)
-        quantize_hg(3)
-        matmul_block(3, 0, (0, 1), 0)
-        matmul_block(3, 1, (0, 1), 3)
-        quantize_h2(3)
-        matmul_block(3, 0, (2,))
-        matmul_block(3, 1, (2,))
+        bias_pair(2)
         sum_shift(0)
         finish_scalar(0, 0)
         finish_scalar(0, 1)
-        bias_pair(2)
+        quantize_hg(3)
         store(0, 0, 2)
+        matmul_block(3, 0, (0, 1), 0)
+        quantize_h2(3)
+        matmul_block(3, 0, (2,))
+        matmul_block(3, 1, (0, 1), 3)
+        matmul_block(3, 1, (2,))
         sum_shift(1)
         finish_scalar(1, 0)
         finish_scalar(1, 1)

@@ -93,7 +93,8 @@ def tile_gin_pc_w4_kernel(
         tsum = sb([P, NB], F32, "tsum")
         shift = sb([P, NB], F32, "shift")
         res = [sb([P, 2, CLS], F32, f"res{i}") for i in range(NP)]
-        h2_grp = [u_grp[1][:], u_grp[0][:], hg_grp[1][:, 0], u_grp[2][:]]
+        h2_grp = [u_grp[1][:], u_grp[0][:], hg_grp[1][:, 0], hg_grp[2][:, 0]]
+        done = [hg_grp[3][:, 0].rearrange("p (b n) t -> p b (n t)", b=2).bitcast(F32)] + res[1:]
 
         u_hbm = u1_bytes.rearrange("(p i b) k -> p i (b k)", i=NP, b=2)
         h_hbm = h.rearrange("(p i b) k -> p i (b k)", i=NP, b=2)
@@ -143,12 +144,6 @@ def tile_gin_pc_w4_kernel(
 
         def negate_nodes():
             nc.scalar.activation(out=node_neg[:], in_=node_x[:], func=IDENT, scale=-1.0)
-
-        def permute_w2_scales():
-            nc.vector.tensor_copy(
-                out=w2s_perm[:].rearrange("p (t m) -> p t m", t=4),
-                in_=w2s_in[:].rearrange("p (m t) -> p t m", t=4),
-            )
 
 
         def cast_scalar(i, b0, b1):
@@ -312,7 +307,7 @@ def tile_gin_pc_w4_kernel(
             )
 
         def store(i, b0, b1):
-            nc.sync.dma_start(out=o_hbm[:, 2 * i + b0 : 2 * i + b1, :], in_=res[i][:, b0:b1, :])
+            nc.sync.dma_start(out=o_hbm[:, 2 * i + b0 : 2 * i + b1, :], in_=done[i][:, b0:b1, :])
 
         warm = zeros[:].bitcast(BF16)
 
@@ -383,6 +378,12 @@ def tile_gin_pc_w4_kernel(
 
         ident_bf = sb([P, P], BF16, "ident_bf")
 
+        def finish_gpsimd(i, b):
+            n = 2 * i + b
+            nc.gpsimd.tensor_scalar(
+                out=done[i][:, b, :], in0=lt_sb[i][:, b, :], scalar1=shift[:, n : n + 1], scalar2=1.0, op0=ADD, op1=MULT
+            )
+
         def turn_block(i, b, step, k):
             bank = take_bank(k, [P, 2, P])
             banks["u", i, b] = bank
@@ -398,6 +399,16 @@ def tile_gin_pc_w4_kernel(
                 op=MULT,
             )
 
+        def permute_w2_scales_half(u):
+            nc.vector.tensor_copy(
+                out=w2s_perm[:, 2 * P * u : 2 * P * (u + 1)].rearrange("p (t m) -> p t m", t=2),
+                in_=w2s_in[:].rearrange("p (m t) -> p t m", t=4)[:, 2 * u : 2 * u + 2, :],
+            )
+
+        def add_log(i):
+            for n in (2 * i, 2 * i + 1):
+                nc.scalar.activation(out=shift[:, n : n + 1], in_=tsum[:, n : n + 1], func=IDENT, bias=shift[:, n : n + 1])
+
         nc.gpsimd.memset(zeros[:], 0.0)
         nc.gpsimd.affine_select(out=ident[:], in_=zeros[:], pattern=[[-1, P]], compare_op=mybir.AluOpType.not_equal, fill=1.0, base=0, channel_multiplier=1)
         nc.vector.memset(w2s_in[:].bitcast(I32), 0)
@@ -407,12 +418,12 @@ def tile_gin_pc_w4_kernel(
         load_u(0)
         load_scale()
         load_u(1)
-        load_h(0)
         load_u(2)
+        load_h(0)
         load_w2()
         load_w2_scales(nc.sync)
-        load_g(0)
         load_u(3)
+        load_g(0)
         load_b2()
         load_h(1)
         load_g(1)
@@ -431,23 +442,25 @@ def tile_gin_pc_w4_kernel(
         cast_sorted(0, 0)
         turn_block(0, 0, 1, 0)
         turn_block(0, 1, 2, 2)
-        turn("h", 0, 3)
-        group("h", 0)
-        cast_scalar(3, 0, 2)
+        warm_up_short(7)
         cast_sorted(1, 0)
         cast_sorted(1, 1)
         turn_sorted(1, 1)
-        warm_up_short(7)
+        turn("h", 0, 3)
         turn("u", 2, 6)
         warm_up_short(7)
+        group("h", 0)
+        cast_scalar(3, 0, 2)
         scale_block(0, 0)
         scale_block(0, 1)
-        permute_w2_scales()
+        permute_w2_scales_half(0)
         quantize_u(0)
-        matmul_h2(0, (4, 5))
-        turn("g", 0, 2)
-        turn("u", 3, 0)
+        matmul_h2_half(0, 0, 4)
         bias_h2(0, 0)
+        permute_w2_scales_half(1)
+        matmul_h2_half(0, 1, 5)
+        turn("u", 3, 0)
+        turn("g", 0, 2)
         bias_h2(0, 1)
         group("g", 0)
         scale_u(1)
@@ -490,36 +503,38 @@ def tile_gin_pc_w4_kernel(
         max_pair(0)
         exp_block(0, 0)
         exp_block(0, 1)
+        offset_max(0)
         log_block(0, 0)
         log_block(0, 1)
-        bias_pair(1)
         quantize_hg(2)
         matmul_pair(2, (0, 1), 6)
+        interleave_gpsimd(3)
         quantize_h2(2)
         matmul_pair(2, (2,))
-        warm_up_short(7)
+        bias_pair(1)
         max_pair(1)
         exp_block(1, 0)
         exp_block(1, 1)
+        offset_max(1)
         log_block(1, 0)
         log_block(1, 1)
-        interleave_vector(3)
+        add_log(0)
+        add_log(1)
+        finish_scalar(1, 0)
+        finish_scalar(1, 1)
         bias_pair(2)
-        sum_shift(0)
-        finish_scalar(0, 0)
-        finish_scalar(0, 1)
+        store(1, 0, 2)
+        warm_up(6)
         quantize_hg(3)
-        store(0, 0, 2)
         matmul_block(3, 0, (0, 1), 0)
+        finish_gpsimd(0, 0)
+        finish_gpsimd(0, 1)
         quantize_h2(3)
+        store(0, 0, 2)
         matmul_block(3, 0, (2,))
         matmul_block(3, 1, (0, 1), 3)
         matmul_block(3, 1, (2,))
-        sum_shift(1)
-        finish_scalar(1, 0)
-        finish_scalar(1, 1)
         max_pair(2)
-        store(1, 0, 2)
         exp_block(2, 0)
         exp_block(2, 1)
         offset_max(2)

@@ -409,6 +409,44 @@ def tile_gin_pc_w4_kernel(
             for n in (2 * i, 2 * i + 1):
                 nc.scalar.activation(out=shift[:, n : n + 1], in_=tsum[:, n : n + 1], func=IDENT, bias=shift[:, n : n + 1])
 
+        def matmul_h2_plane(i, t, k):
+            bank = take_bank(k, [P, 256])
+            banks["plane", i, t] = bank
+            nc.tensor.matmul_mx(
+                out=bank[:],
+                lhsT=w2_perm[:, 2 * P * t : 2 * P * (t + 1)].bitcast(FP4X4),
+                lhsT_scale=w2s_perm[:, P * t : P * (t + 1)],
+                rhs=u_codes[i][:].bitcast(FP8X4),
+                rhs_scale=u_scl[i][:],
+                start=True,
+                stop=True,
+            )
+
+        def scale_part(i, n0, n1):
+            nodes = slice(n0, n1)
+            nc.vector.tensor_tensor(
+                out=u_grp[i][:, nodes, :].rearrange("p n (e j) -> p n e j", e=2),
+                in0=banks["u", i][:, :, nodes].bitcast(BF16).rearrange("p e (n j) -> p n e j", j=2),
+                in1=scale_col[:].rearrange("p (e j) -> p e j", e=2).unsqueeze(1).to_broadcast([P, n1 - n0, 2, 2]),
+                op=MULT,
+            )
+
+        def bias_half(i, b):
+            nc.vector.tensor_tensor(out=lt_sb[i][:, b, :], in0=banks["rows", i][:, b, :], in1=bo_all[:], op=ADD)
+
+        def interleave_gpsimd_part(i, n0, n1):
+            nc.gpsimd.tensor_scalar(
+                out=h2_grp[i][:, n0:n1, :],
+                in0=planes[i][:, :, n0:n1].rearrange("p t n -> p n t"),
+                scalar1=1.0,
+                scalar2=0.0,
+                op0=MULT,
+                op1=ADD,
+            )
+
+        def interleave_vector_part(i, n0, n1):
+            nc.vector.tensor_copy(out=h2_grp[i][:, n0:n1, :], in_=planes[i][:, :, n0:n1].rearrange("p t n -> p n t"))
+
         nc.gpsimd.memset(zeros[:], 0.0)
         nc.gpsimd.affine_select(out=ident[:], in_=zeros[:], pattern=[[-1, P]], compare_op=mybir.AluOpType.not_equal, fill=1.0, base=0, channel_multiplier=1)
         nc.vector.memset(w2s_in[:].bitcast(I32), 0)
@@ -461,20 +499,21 @@ def tile_gin_pc_w4_kernel(
         matmul_h2_half(0, 1, 5)
         turn("u", 3, 0)
         turn("g", 0, 2)
+        turn("h", 1, 3)
         bias_h2(0, 1)
         group("g", 0)
+        group("h", 1)
         scale_u(1)
+        scale_part(2, 0, 64)
         quantize_u(1)
-        matmul_h2(1, (3, 7))
-        turn("h", 1, 1)
+        matmul_h2(1, (1, 7))
         turn("g", 1, 4)
         turn("h", 2, 5)
         bias_h2(1, 0)
         bias_h2(1, 1)
-        group("h", 1)
         group("g", 1)
         interleave_gpsimd(0)
-        scale_u(2)
+        scale_part(2, 64, 256)
         scale_u(3)
         quantize_u(2)
         matmul_h2(2, (2, 6))
@@ -492,28 +531,33 @@ def tile_gin_pc_w4_kernel(
         bias_h2(3, 1)
         interleave_vector(1)
         quantize_hg(1)
-        interleave_gpsimd(2)
+        interleave_gpsimd_part(2, 0, 160)
         quantize_h2(1)
         matmul_pair(1, (0, 1, 2), 4)
         turn("h", 3, 5)
         turn("g", 3, 2)
         group("h", 3)
         group("g", 3)
-        bias_pair(0)
-        max_pair(0)
+        bias_half(0, 0)
+        bias_half(0, 1)
+        max_block(0, 0)
         exp_block(0, 0)
+        max_block(0, 1)
         exp_block(0, 1)
         offset_max(0)
         log_block(0, 0)
         log_block(0, 1)
+        interleave_vector_part(2, 160, 256)
         quantize_hg(2)
         matmul_pair(2, (0, 1), 6)
         interleave_gpsimd(3)
         quantize_h2(2)
         matmul_pair(2, (2,))
-        bias_pair(1)
-        max_pair(1)
+        bias_half(1, 0)
+        bias_half(1, 1)
+        max_block(1, 0)
         exp_block(1, 0)
+        max_block(1, 1)
         exp_block(1, 1)
         offset_max(1)
         log_block(1, 0)

@@ -455,6 +455,7 @@ def tile_gin_pc_w4_kernel(
         make_nodes()
         load_u(0)
         load_scale()
+        load_b2()
         load_u(1)
         load_u(2)
         load_h(0)
@@ -462,12 +463,11 @@ def tile_gin_pc_w4_kernel(
         load_w2_scales(nc.sync)
         load_u(3)
         load_g(0)
-        load_b2()
         load_h(1)
         load_g(1)
+        load_h(2)
         load_wo()
         load_wo_scales(nc.sync)
-        load_h(2)
         load_g(2)
         load_bo()
         load_h(3)

import math
from contextlib import ExitStack

import concourse.mybir as mybir

FLOPS = 2 * 1024 * 512 * 512 + 2 * 1024 * 1536 * 256

F32 = mybir.dt.float32
BF16 = mybir.dt.bfloat16
I32 = mybir.dt.int32
U32 = mybir.dt.uint32
U16 = mybir.dt.uint16
U8 = mybir.dt.uint8
FP8 = mybir.dt.float8_e4m3fn
FP8X4 = mybir.dt.float8_e4m3fn_x4
FP4X4 = mybir.dt.float4_e2m1fn_x4
ADD = mybir.AluOpType.add
MULT = mybir.AluOpType.mult
MAX = mybir.AluOpType.max
AX = mybir.AxisListType.X
EXP = mybir.ActivationFunctionType.Exp
IDENT = mybir.ActivationFunctionType.Identity

P = 128
NODES, HID, CLS = 1024, 512, 256
NB = NODES // P
NP = NB // 2

LOG_STEP = -0.875
STEP = math.exp(LOG_STEP)
TERMS = 50
T0 = 3.25 - (TERMS - 1) * STEP
T_TAIL = T0 + STEP - math.log(math.exp(STEP) - 1.0)
LOG_CONST = STEP * (math.exp(-math.exp(T_TAIL)) + sum(math.exp(-math.exp(T0 + j * STEP)) for j in range(1, TERMS)))

U_LOADS = ((0, 1), (1, 1), (2, 1), (3, 1))
H_LOADS = ((0, 1), (1, 1), (2, 1), (3, 1))
G_LOADS = ((0, 1), (1, 1), (2, 1), (3, 1))


def tile_gin_pc_w4_kernel(
    tc, u1_bytes, u1_scale, w2_words, w2_scales, b2_1, h, h1, wo_words, wo_scales, b_out, out
):
    nc = tc.nc
    with ExitStack() as ctx:
        keep = ctx.enter_context(tc.tile_pool(name="keep", bufs=1))
        psum = ctx.enter_context(tc.psum_pool(name="psum", bufs=1))
        ctx.enter_context(tc.manual_schedule())

        def sb(shape, dtype, name):
            return keep.tile(shape, dtype, name=name, align_bytes=64)

        def take_bank(k, shape):
            return psum.tile(shape, F32, name=f"bank{k}", tag=f"bank{k}")

        scale_col = sb([P, 4], F32, "scale_col")
        b2_col = sb([P, 4], BF16, "b2_col")
        u_raw = {i: sb([P, n, 2 * HID], U8, f"u_raw{i}") for i, n in U_LOADS}
        h_sb = {i: sb([P, n, HID], F32, f"h_sb{i}") for i, n in H_LOADS}
        g_sb = {i: sb([P, n, HID], F32, f"g_sb{i}") for i, n in G_LOADS}

        def pair_of(tiles, loads, i):
            first = max(f for f, n in loads if f <= i)
            return tiles[first][:, i - first, :]

        w2_in = sb([P, 2 * HID], U8, "w2_in")
        w2_perm = sb([P, 2 * HID], U8, "w2_perm")
        w2s_in = sb([P, HID], U8, "w2s_in")
        w2s_perm = sb([P, HID], U8, "w2s_perm")
        wo = sb([P, 3, 2 * CLS], U8, "wo")
        wos = sb([P, 3, CLS], U8, "wos")
        zeros = sb([P, P], F32, "zeros")
        ident = sb([P, P], F32, "ident")
        ones = sb([P, TERMS], F32, "ones")
        count = sb([P, TERMS], F32, "count")
        node_x = sb([P, TERMS], F32, "node_x")
        node_neg = sb([P, TERMS], F32, "node_neg")
        u_wide = [sb([P, 2 * HID], BF16, f"u_wide{i}") for i in range(NP)]
        u_grp = [sb([P, 256, 4], BF16, f"u_grp{i}") for i in range(NP)]
        hg_grp = [sb([P, 2, 256, 4], BF16, f"hg_grp{i}") for i in range(NP)]
        u_codes = [sb([P, 256], U32, f"u_codes{i}") for i in range(NP)]
        u_scl = [sb([P, 256], U8, f"u_scl{i}") for i in range(NP)]
        hg_codes = [sb([P, 512], U32, f"hg_codes{i}") for i in range(NP)]
        hg_scl = [sb([P, 512], U8, f"hg_scl{i}") for i in range(NP)]
        h2_codes = [sb([P, 256], U32, f"h2_codes{i}") for i in range(NP)]
        h2_scl = [sb([P, 256], U8, f"h2_scl{i}") for i in range(NP)]
        planes = [sb([P, 4, 256], BF16, f"planes{i}") for i in range(NP)]
        bo_all = sb([P, CLS], BF16, "bo_all")
        lt_sb = [sb([P, 2, 256], F32, f"lt_sb{i}") for i in range(NP)]
        terms = [sb([P, TERMS], F32, f"terms{n}") for n in range(NB)]
        nmax = sb([P, NB], F32, "nmax")
        ssum = sb([P, NB], F32, "ssum")
        tsum = sb([P, NB], F32, "tsum")
        shift = sb([P, NB], F32, "shift")
        res = [sb([P, 2, CLS], F32, f"res{i}") for i in range(NP)]
        h2_grp = [u_grp[1][:], u_grp[0][:], hg_grp[1][:, 0], hg_grp[2][:, 0]]
        done = [hg_grp[3][:, 0].rearrange("p (b n) t -> p b (n t)", b=2).bitcast(F32)] + res[1:]

        u_hbm = u1_bytes.rearrange("(p i b) k -> p i (b k)", i=NP, b=2)
        h_hbm = h.rearrange("(p i b) k -> p i (b k)", i=NP, b=2)
        g_hbm = h1.rearrange("(p i b) k -> p i (b k)", i=NP, b=2)
        o_hbm = out.rearrange("(p b) c -> p b c", b=NB)

        def load_u(i):
            nc.sync.dma_start(out=u_raw[i][:], in_=u_hbm[:, i : i + dict(U_LOADS)[i], :])

        def load_h(i):
            nc.sync.dma_start(out=h_sb[i][:], in_=h_hbm[:, i : i + dict(H_LOADS)[i], :].bitcast(F32))

        def load_g(i):
            nc.sync.dma_start(out=g_sb[i][:], in_=g_hbm[:, i : i + dict(G_LOADS)[i], :].bitcast(F32))

        def load_scale():
            nc.sync.dma_start(out=scale_col[:], in_=u1_scale.rearrange("o (p j) -> p (o j)", j=4))

        def load_w2():
            nc.sync.dma_start(out=w2_in[:], in_=w2_words[0])

        def load_b2():
            nc.sync.dma_start(out=b2_col[:], in_=b2_1.rearrange("(p t) -> p t", t=4))

        def load_wo():
            nc.sync.dma_start(out=wo[:], in_=wo_words.rearrange("g p n -> p g n"))

        def load_bo():
            nc.sync.dma_start(out=bo_all[:], in_=b_out.partition_broadcast(P))

        def load_w2_scales(queue):
            w2s_hbm = w2_scales[0].rearrange("(q r) n -> r q n", r=4)
            for r in range(4):
                queue.dma_start(out=w2s_in[r:P:32, :].bitcast(I32), in_=w2s_hbm[r].bitcast(I32))

        def load_wo_scales(queue):
            wos_hbm = wo_scales.rearrange("g (q r) n -> r q g n", r=4)
            for r in range(4):
                queue.dma_start(out=wos[r:P:32, :, :].bitcast(I32), in_=wos_hbm[r].bitcast(I32))

        banks = {}

        def make_nodes():
            nc.scalar.activation(out=node_x[:, 0:1], in_=ones[:, 0:1], func=EXP, scale=T_TAIL)
            nc.vector.tensor_tensor_scan(out=count[:], data0=ones[:], data1=ones[:], initial=-1.0, op0=MULT, op1=ADD)
            nc.scalar.activation(out=node_x[:, 1:], in_=count[:, 1:], func=EXP, scale=STEP, bias=T0)

        def negate_nodes():
            nc.scalar.activation(out=node_neg[:], in_=node_x[:], func=IDENT, scale=-1.0)


        def cast_scalar(i, b0, b1):
            cols = slice(b0 * HID, b1 * HID)
            nc.scalar.copy(out=u_wide[i][:, cols], in_=pair_of(u_raw, U_LOADS, i)[:, cols].bitcast(FP8))

        def cast_vector(i, b0, b1):
            cols = slice(b0 * HID, b1 * HID)
            nc.vector.tensor_copy(out=u_wide[i][:, cols], in_=pair_of(u_raw, U_LOADS, i)[:, cols].bitcast(FP8))

        def turn(x, i, k):
            bank = take_bank(k, [P, 2, 2 * P])
            banks[x, i] = bank
            if x == "u":
                rows = u_wide[i][:].bitcast(F32)
            else:
                rows = pair_of(h_sb, H_LOADS, i) if x == "h" else pair_of(g_sb, G_LOADS, i)
            for b in range(2):
                for e in range(2):
                    nc.tensor.transpose(bank[:, e, b * P : (b + 1) * P], rows[:, b * 256 + e : (b + 1) * 256 : 2], ident[:])

        def scale_u(i):
            nc.vector.tensor_tensor(
                out=u_grp[i][:].rearrange("p n (e j) -> p n e j", e=2),
                in0=banks["u", i][:].bitcast(BF16).rearrange("p e (n j) -> p n e j", j=2),
                in1=scale_col[:].rearrange("p (e j) -> p e j", e=2).unsqueeze(1).to_broadcast([P, 256, 2, 2]),
                op=MULT,
            )

        def grouped_words(x, i):
            return hg_grp[i][:, 0 if x == "h" else 1].bitcast(F32)

        def group(x, i):
            nc.scalar.copy(out=grouped_words(x, i), in_=banks[x, i][:].rearrange("p e n -> p n e"))

        def quantize(codes, scl, grp):
            nc.vector.quantize_mx(out=codes[:].bitcast(FP8X4), scales=scl[:], in_=grp)

        def quantize_u(i):
            quantize(u_codes[i], u_scl[i], u_grp[i][:].rearrange("p n t -> p (n t)"))

        def quantize_hg(i):
            quantize(hg_codes[i], hg_scl[i], hg_grp[i][:].rearrange("p s n t -> p (s n t)"))

        def quantize_h2(i):
            quantize(h2_codes[i], h2_scl[i], h2_grp[i].rearrange("p n t -> p (n t)"))

        def matmul_h2(i, k):
            for u in range(2):
                bank = take_bank(k[u], [P, 2, 256])
                banks["h2", i, u] = bank
                for v in range(2):
                    t = 2 * u + v
                    nc.tensor.matmul_mx(
                        out=bank[:, v, :],
                        lhsT=w2_perm[:, 2 * P * t : 2 * P * (t + 1)].bitcast(FP4X4),
                        lhsT_scale=w2s_perm[:, P * t : P * (t + 1)],
                        rhs=u_codes[i][:].bitcast(FP8X4),
                        rhs_scale=u_scl[i][:],
                        start=True,
                        stop=True,
                    )

        def bias_h2(i, u):
            for v in range(2):
                t = 2 * u + v
                nc.scalar.activation(
                    out=planes[i][:, t, :], in_=banks["h2", i, u][:, v, :], func=IDENT, bias=b2_col[:, t : t + 1]
                )

        def interleave_vector(i):
            nc.vector.tensor_copy(out=h2_grp[i], in_=planes[i][:].rearrange("p t n -> p n t"))

        def interleave_gpsimd(i):
            nc.gpsimd.tensor_scalar(
                out=h2_grp[i], in0=planes[i][:].rearrange("p t n -> p n t"), scalar1=1.0, scalar2=0.0, op0=MULT, op1=ADD
            )

        def matmul_pair(i, groups, k=None):
            if groups[0] == 0:
                banks["rows", i] = take_bank(k, [P, 2, CLS])
            for g in groups:
                codes, scl = (hg_codes[i], hg_scl[i]) if g < 2 else (h2_codes[i], h2_scl[i])
                for b in range(2):
                    nodes = slice(256 * (g % 2) + b * P, 256 * (g % 2) + (b + 1) * P)
                    nc.tensor.matmul_mx(
                        out=banks["rows", i][:, b, :],
                        lhsT=codes[:, nodes].bitcast(FP8X4),
                        lhsT_scale=scl[:, nodes],
                        rhs=wo[:, g, :].bitcast(FP4X4),
                        rhs_scale=wos[:, g, :],
                        start=(g == 0 and b == 0),
                        stop=(g == 2 and b == 1),
                    )

        def matmul_block(i, b, groups, k=None):
            if groups[0] == 0:
                banks["rows", i, b] = take_bank(k, [P, CLS])
            for g in groups:
                codes, scl = (hg_codes[i], hg_scl[i]) if g < 2 else (h2_codes[i], h2_scl[i])
                nodes = slice(256 * (g % 2) + b * P, 256 * (g % 2) + (b + 1) * P)
                nc.tensor.matmul_mx(
                    out=banks["rows", i, b][:],
                    lhsT=codes[:, nodes].bitcast(FP8X4),
                    lhsT_scale=scl[:, nodes],
                    rhs=wo[:, g, :].bitcast(FP4X4),
                    rhs_scale=wos[:, g, :],
                    start=(g == 0),
                    stop=(g == 2),
                )

        def bias_pair(i):
            nc.vector.tensor_tensor(
                out=lt_sb[i][:], in0=banks["rows", i][:], in1=bo_all[:].unsqueeze(1).to_broadcast([P, 2, CLS]), op=ADD
            )

        def max_pair(i):
            nc.vector.tensor_reduce(out=nmax[:, 2 * i : 2 * i + 2], in_=lt_sb[i][:], axis=AX, op=MAX, negate=True)

        def offset_max(i):
            cols = slice(2 * i, 2 * i + 2)
            nc.scalar.activation(out=shift[:, cols], in_=nmax[:, cols], func=IDENT, bias=-LOG_CONST)

        def bias_block(i, b):
            nc.vector.tensor_tensor(out=lt_sb[i][:, b, :], in0=banks["rows", i, b][:], in1=bo_all[:], op=ADD)

        def max_block(i, b):
            n = 2 * i + b
            nc.vector.tensor_reduce(out=nmax[:, n : n + 1], in_=lt_sb[i][:, b, :], axis=AX, op=MAX, negate=True)

        def exp_block(i, b):
            n = 2 * i + b
            nc.scalar.activation(
                out=res[i][:, b, :],
                in_=lt_sb[i][:, b, :],
                func=EXP,
                bias=nmax[:, n : n + 1],
                accum_out=ssum[:, n : n + 1],
            )

        def log_block(i, b):
            n = 2 * i + b
            nc.scalar.activation(
                out=terms[n][:],
                in_=node_neg[:],
                func=EXP,
                scale=ssum[:, n : n + 1],
                bias=LOG_STEP,
                accum_out=tsum[:, n : n + 1],
            )

        def finish_block(i, b):
            n = 2 * i + b
            nc.vector.tensor_scalar(
                out=res[i][:, b, :],
                in0=lt_sb[i][:, b, :],
                scalar1=shift[:, n : n + 1],
                scalar2=tsum[:, n : n + 1],
                op0=ADD,
                op1=ADD,
            )

        def store(i, b0, b1):
            nc.sync.dma_start(out=o_hbm[:, 2 * i + b0 : 2 * i + b1, :], in_=done[i][:, b0:b1, :])

        warm = zeros[:].bitcast(BF16)

        def warm_up_first(count, k):
            bank = take_bank(k, [P, 2, 2 * P])
            moving = warm.unsqueeze(1).to_broadcast([P, 2, 2 * P])
            for step in range(count):
                nc.tensor.matmul(bank[:], lhsT=warm[:, :P], rhs=moving, start=True, stop=True)

        def warm_up(k):
            bank = take_bank(k, [P, 2, P])
            words = zeros[:]
            nc.tensor.matmul(bank[:], lhsT=words, rhs=words.unsqueeze(1).to_broadcast([P, 2, P]), start=True, stop=True)

        def warm_up_short(k):
            bank = take_bank(k, [P, P])
            words = zeros[:]
            nc.tensor.matmul(bank[:], lhsT=words, rhs=words, start=True, stop=True)

        def matmul_h2_half(i, u, k):
            bank = take_bank(k, [P, 2, 256])
            banks["h2", i, u] = bank
            for v in range(2):
                t = 2 * u + v
                nc.tensor.matmul_mx(
                    out=bank[:, v, :],
                    lhsT=w2_perm[:, 2 * P * t : 2 * P * (t + 1)].bitcast(FP4X4),
                    lhsT_scale=w2s_perm[:, P * t : P * (t + 1)],
                    rhs=u_codes[i][:].bitcast(FP8X4),
                    rhs_scale=u_scl[i][:],
                    start=True,
                    stop=True,
                )

        def cast_sorted(i, b):
            nc.vector.tensor_scalar(
                out=u_wide[i][:, b * HID : (b + 1) * HID].rearrange("p (e m j) -> p m e j", e=2, j=2),
                in0=pair_of(u_raw, U_LOADS, i)[:, b * HID : (b + 1) * HID].bitcast(FP8),
                scalar1=ones[:, 0:1],
                scalar2=None,
                op0=MULT,
            )

        def turn_sorted(i, k):
            bank = take_bank(k, [P, 2, 2 * P])
            banks["u", i] = bank
            words = u_wide[i][:].bitcast(F32)
            for b in range(2):
                for e in range(2):
                    first = (2 * b + e) * P
                    nc.tensor.transpose(bank[:, e, b * P : (b + 1) * P], words[:, first : first + P], ident[:])

        def permute_w2_words_scalar():
            nc.scalar.copy(
                out=w2_perm[:].bitcast(U16).rearrange("p (t m) -> p t m", t=4),
                in_=w2_in[:].bitcast(U16).rearrange("p (m t) -> p t m", t=4),
            )

        def sum_shift(i):
            cols = slice(2 * i, 2 * i + 2)
            nc.vector.scalar_tensor_tensor(
                out=shift[:, cols], in0=nmax[:, cols], scalar=-LOG_CONST, in1=tsum[:, cols], op0=ADD, op1=ADD
            )

        def finish_scalar(i, b):
            n = 2 * i + b
            nc.scalar.activation(out=res[i][:, b, :], in_=lt_sb[i][:, b, :], func=IDENT, bias=shift[:, n : n + 1])

        ident_bf = sb([P, P], BF16, "ident_bf")

        def finish_gpsimd(i, b):
            n = 2 * i + b
            nc.gpsimd.tensor_scalar(
                out=done[i][:, b, :], in0=lt_sb[i][:, b, :], scalar1=shift[:, n : n + 1], scalar2=1.0, op0=ADD, op1=MULT
            )

        def turn_block(i, b, step, k):
            bank = take_bank(k, [P, 2, P])
            banks["u", i, b] = bank
            words = u_wide[i][:, b * HID : (b + 1) * HID].bitcast(F32)
            for e in range(2):
                nc.tensor.transpose(bank[:, e, :], words[:, e:256:2] if step == 2 else words[:, e * P : (e + 1) * P], ident[:])

        def scale_block(i, b):
            nc.vector.tensor_tensor(
                out=u_grp[i][:, b * P : (b + 1) * P, :].rearrange("p n (e j) -> p n e j", e=2),
                in0=banks["u", i, b][:].bitcast(BF16).rearrange("p e (n j) -> p n e j", j=2),
                in1=scale_col[:].rearrange("p (e j) -> p e j", e=2).unsqueeze(1).to_broadcast([P, P, 2, 2]),
                op=MULT,
            )

        def permute_w2_scales_half(u):
            nc.vector.tensor_copy(
                out=w2s_perm[:, 2 * P * u : 2 * P * (u + 1)].rearrange("p (t m) -> p t m", t=2),
                in_=w2s_in[:].rearrange("p (m t) -> p t m", t=4)[:, 2 * u : 2 * u + 2, :],
            )

        def add_log(i):
            for n in (2 * i, 2 * i + 1):
                nc.scalar.activation(out=shift[:, n : n + 1], in_=tsum[:, n : n + 1], func=IDENT, bias=shift[:, n : n + 1])

        def matmul_h2_plane(i, t, k):
            bank = take_bank(k, [P, 256])
            banks["plane", i, t] = bank
            nc.tensor.matmul_mx(
                out=bank[:],
                lhsT=w2_perm[:, 2 * P * t : 2 * P * (t + 1)].bitcast(FP4X4),
                lhsT_scale=w2s_perm[:, P * t : P * (t + 1)],
                rhs=u_codes[i][:].bitcast(FP8X4),
                rhs_scale=u_scl[i][:],
                start=True,
                stop=True,
            )

        def scale_part(i, n0, n1):
            nodes = slice(n0, n1)
            nc.vector.tensor_tensor(
                out=u_grp[i][:, nodes, :].rearrange("p n (e j) -> p n e j", e=2),
                in0=banks["u", i][:, :, nodes].bitcast(BF16).rearrange("p e (n j) -> p n e j", j=2),
                in1=scale_col[:].rearrange("p (e j) -> p e j", e=2).unsqueeze(1).to_broadcast([P, n1 - n0, 2, 2]),
                op=MULT,
            )

        def bias_half(i, b):
            nc.vector.tensor_tensor(out=lt_sb[i][:, b, :], in0=banks["rows", i][:, b, :], in1=bo_all[:], op=ADD)

        def interleave_gpsimd_part(i, n0, n1):
            nc.gpsimd.tensor_scalar(
                out=h2_grp[i][:, n0:n1, :],
                in0=planes[i][:, :, n0:n1].rearrange("p t n -> p n t"),
                scalar1=1.0,
                scalar2=0.0,
                op0=MULT,
                op1=ADD,
            )

        def interleave_vector_part(i, n0, n1):
            nc.vector.tensor_copy(out=h2_grp[i][:, n0:n1, :], in_=planes[i][:, :, n0:n1].rearrange("p t n -> p n t"))

        nc.gpsimd.memset(zeros[:], 0.0)
        nc.gpsimd.affine_select(out=ident[:], in_=zeros[:], pattern=[[-1, P]], compare_op=mybir.AluOpType.not_equal, fill=1.0, base=0, channel_multiplier=1)
        nc.vector.memset(w2s_in[:].bitcast(I32), 0)
        nc.vector.memset(ones[:], 1.0)
        nc.vector.memset(wos[:].rearrange("p g n -> p (g n)").bitcast(I32), 0)
        make_nodes()
        load_u(0)
        load_scale()
        load_b2()
        load_u(1)
        load_u(2)
        load_h(0)
        load_w2()
        load_w2_scales(nc.sync)
        load_u(3)
        load_g(0)
        load_h(1)
        load_g(1)
        load_h(2)
        load_wo()
        load_wo_scales(nc.sync)
        load_g(2)
        load_bo()
        load_h(3)
        load_g(3)
        warm_up_first(4, 7)
        cast_scalar(0, 1, 2)
        negate_nodes()
        cast_scalar(2, 0, 2)
        permute_w2_words_scalar()
        cast_sorted(0, 0)
        turn_block(0, 0, 1, 0)
        turn_block(0, 1, 2, 2)
        warm_up_short(7)
        cast_sorted(1, 0)
        cast_sorted(1, 1)
        turn_sorted(1, 1)
        turn("h", 0, 3)
        turn("u", 2, 6)
        warm_up_short(7)
        group("h", 0)
        cast_scalar(3, 0, 2)
        scale_block(0, 0)
        scale_block(0, 1)
        permute_w2_scales_half(0)
        quantize_u(0)
        matmul_h2_half(0, 0, 4)
        bias_h2(0, 0)
        permute_w2_scales_half(1)
        matmul_h2_half(0, 1, 5)
        turn("u", 3, 0)
        turn("g", 0, 2)
        turn("h", 1, 3)
        bias_h2(0, 1)
        group("g", 0)
        group("h", 1)
        scale_u(1)
        scale_part(2, 0, 64)
        quantize_u(1)
        matmul_h2(1, (1, 7))
        turn("g", 1, 4)
        turn("h", 2, 5)
        bias_h2(1, 0)
        bias_h2(1, 1)
        group("g", 1)
        interleave_gpsimd(0)
        scale_part(2, 64, 256)
        scale_u(3)
        quantize_u(2)
        matmul_h2(2, (2, 6))
        bias_h2(2, 0)
        bias_h2(2, 1)
        group("h", 2)
        quantize_hg(0)
        quantize_h2(0)
        matmul_pair(0, (0, 1, 2), 0)
        turn("g", 2, 3)
        group("g", 2)
        quantize_u(3)
        matmul_h2(3, (7, 1))
        bias_h2(3, 0)
        bias_h2(3, 1)
        interleave_vector(1)
        quantize_hg(1)
        interleave_gpsimd_part(2, 0, 160)
        quantize_h2(1)
        matmul_pair(1, (0, 1, 2), 4)
        turn("h", 3, 5)
        turn("g", 3, 2)
        group("h", 3)
        group("g", 3)
        bias_half(0, 0)
        bias_half(0, 1)
        max_block(0, 0)
        exp_block(0, 0)
        max_block(0, 1)
        exp_block(0, 1)
        offset_max(0)
        log_block(0, 0)
        log_block(0, 1)
        interleave_vector_part(2, 160, 256)
        quantize_hg(2)
        matmul_pair(2, (0, 1), 6)
        interleave_gpsimd(3)
        quantize_h2(2)
        matmul_pair(2, (2,))
        bias_half(1, 0)
        bias_half(1, 1)
        max_block(1, 0)
        exp_block(1, 0)
        max_block(1, 1)
        exp_block(1, 1)
        offset_max(1)
        log_block(1, 0)
        log_block(1, 1)
        add_log(0)
        add_log(1)
        finish_scalar(1, 0)
        finish_scalar(1, 1)
        bias_pair(2)
        store(1, 0, 2)
        warm_up(6)
        quantize_hg(3)
        matmul_block(3, 0, (0, 1), 0)
        finish_gpsimd(0, 0)
        finish_gpsimd(0, 1)
        quantize_h2(3)
        store(0, 0, 2)
        matmul_block(3, 0, (2,))
        matmul_block(3, 1, (0, 1), 3)
        matmul_block(3, 1, (2,))
        max_pair(2)
        exp_block(2, 0)
        exp_block(2, 1)
        offset_max(2)
        log_block(2, 0)
        log_block(2, 1)
        bias_block(3, 0)
        bias_block(3, 1)
        max_block(3, 0)
        exp_block(3, 0)
        max_block(3, 1)
        exp_block(3, 1)
        offset_max(3)
        log_block(3, 0)
        log_block(3, 1)
        finish_block(2, 0)
        finish_block(2, 1)
        store(2, 0, 2)
        finish_block(3, 0)
        store(3, 0, 1)
        finish_block(3, 1)
        store(3, 1, 2)
